import numpy as np
import ml_dtypes


def mxq(x, axis, fmt="e4m3"):
    dtype, down = {"e4m3": (ml_dtypes.float8_e4m3fn, 7), "e5m2": (ml_dtypes.float8_e5m2, 14)}[fmt]
    v = np.moveaxis(np.asarray(x, np.float32).astype(ml_dtypes.bfloat16).astype(np.float64), axis, -1)
    blocks = v.reshape(v.shape[:-1] + (-1, 32))
    amax = np.abs(blocks).max(-1, keepdims=True)
    byte = np.maximum(np.where(amax > 0, np.frexp(amax)[1] - 1 + 127, 0) - down, 1)
    scale = np.exp2(byte - 127.0)
    codes = (blocks / scale).astype(np.float32).astype(dtype).astype(np.float64)
    return np.moveaxis((codes * scale).reshape(v.shape), -1, axis)


WIDE = False


def mx_kscale(k):
    if not WIDE:
        return np.ones(k)
    levels = np.array([10, -10, 5, -5, 0])
    a = np.random.permutation(np.resize(levels, k // 512 * 4)).reshape(k // 512, 4)
    idx = np.arange(k)
    return np.exp2(a[idx // 512, idx % 128 // 32])


BF16 = ml_dtypes.bfloat16


def bf(x):
    return np.asarray(x, np.float32).astype(BF16)


def f64(x):
    return np.asarray(x).astype(np.float64)


K, D, H, R, V, B, T = 4, 1024, 2048, 1024, 2052, 4, 64
LN_EPS = 1e-5
ERF_CAP = 6.0
ERF_TERMS = 100


def erf(v):
    a = np.minimum(np.abs(v), ERF_CAP)
    term = a.copy()
    total = a.copy()
    for n in range(ERF_TERMS):
        term = term * (a * a) / (n + 1.5)
        total = total + term
    return np.sign(v) * total * np.exp(-a * a) / np.sqrt(0.25 * np.pi)


def gelu(v):
    return 0.5 * v * (1.0 + erf(v * np.sqrt(0.5)))


def setup_inputs():
    s = mx_kscale(D)
    amp = np.exp2(-9.0 * np.random.random((B, T, 1)))
    x = amp * (np.random.standard_normal((B, T, D)) + 0.5 * np.random.standard_normal((B, T, 1)))
    return {"x": bf(x),
            "ln_scale": bf((1.0 + 0.2 * np.random.standard_normal((K, D))) * s),
            "ln_bias": bf(0.2 * np.random.standard_normal((K, D)) * s),
            "W1": bf(np.random.standard_normal((K, D, H)) / np.sqrt(D) / s[None, :, None]),
            "b1": bf(0.3 * np.random.standard_normal((K, H)))}


def reference(x, ln_scale, ln_bias, W1, b1):
    x = f64(x)
    mu = x.mean(-1, keepdims=True)
    var = np.square(x - mu).mean(-1, keepdims=True)
    xn = (x - mu) / np.sqrt(var + LN_EPS)
    y = xn[:, None, :, :] * f64(ln_scale)[None, :, None, :] + f64(ln_bias)[None, :, None, :]
    return gelu((mxq(y, 3, "e4m3") @ mxq(f64(W1), 1, "e4m3")) + f64(b1)[None, :, None, :])

@@ -1,0 +1,260 @@
+from contextlib import ExitStack
+
+import concourse.mybir as mybir
+from concourse.masks import make_identity
+
+F32 = mybir.dt.float32
+BF16 = mybir.dt.bfloat16
+U32 = mybir.dt.uint32
+U8 = mybir.dt.uint8
+I32 = mybir.dt.int32
+FP8X4 = mybir.dt.float8_e4m3fn_x4
+ACT = mybir.ActivationFunctionType
+ALU = mybir.AluOpType
+
+P = 128
+HEADS, D, H, BATCH, T = 4, 1024, 2048, 4, 64
+LN_EPS = 1e-5
+PASSES = 2
+NBLK = 512
+ROUNDS_PER_HEAD = H // NBLK
+ROUNDS = HEADS * ROUNDS_PER_HEAD
+TOK = BATCH * T
+
+FLOPS = 2 * TOK * D * H * HEADS
+
+S_COLS = [512, 512, 256] + [128] * 11 + [64, 0]
+V_OUT_FROM = 14
+RAW_BUFS = 6
+HEAD0_SPLITS = [(0, 512), (512, 1024), (1024, 2048)]
+
+
+def tile_twostepvoicecraftheads_pa_kernel(tc, x, ln_scale, ln_bias, W1, b1, out):
+    nc = tc.nc
+    with ExitStack() as ctx:
+        const = ctx.enter_context(tc.tile_pool(name="const", bufs=1))
+        rawp = ctx.enter_context(tc.tile_pool(name="rawp", bufs=RAW_BUFS))
+        wgp = ctx.enter_context(tc.tile_pool(name="wgp", bufs=3))
+        wcp = ctx.enter_context(tc.tile_pool(name="wcp", bufs=4))
+        yp = ctx.enter_context(tc.tile_pool(name="yp", bufs=2))
+        gp = ctx.enter_context(tc.tile_pool(name="gp", bufs=3))
+        op = ctx.enter_context(tc.tile_pool(name="op", bufs=5))
+        psa = ctx.enter_context(tc.psum_pool(name="psa", bufs=4))
+        pst = ctx.enter_context(tc.psum_pool(name="pst", bufs=4))
+
+        ident = const.tile([P, P], F32, name="ident")
+        make_identity(nc, ident[:])
+        identb = const.tile([P, P], BF16, name="identb")
+        nc.vector.tensor_copy(out=identb[:], in_=ident[:])
+        neghalf = const.tile([P, 2], F32, name="neghalf")
+        nc.vector.memset(neghalf[:], -0.5)
+        warm = const.tile([P, 1], F32, name="warm")
+        nc.vector.memset(warm[:], 0.0)
+        prm = const.tile([P, 640], BF16, name="prm")
+        nc.vector.memset(prm[:].bitcast(I32), 0)
+
+        xt = const.tile([P, 2, D], BF16, name="xt")
+        xv = x.rearrange("(m e) t d -> e t m d", e=2)
+        for e in range(2):
+            nc.sync.dma_start(out=xt[e:P:2, :, :], in_=xv[e])
+        nc.scalar.dma_start(out=prm[0:8, 0:512], in_=ln_scale.rearrange("k (g c) -> (k g) c", g=2))
+        nc.scalar.dma_start(out=prm[8:16, 0:512], in_=ln_bias.rearrange("k (g c) -> (k g) c", g=2))
+        nc.scalar.dma_start(out=prm[0:64, 512:640], in_=b1.rearrange("k (a j) -> (k a) j", j=P))
+
+        warm2 = const.tile([P, 1], F32, name="warm2")
+        nc.scalar.activation(out=warm2[:], in_=warm[:], func=ACT.Gelu)
+
+        raw = {}
+
+        def load_w(k, splits):
+            for g in range(PASSES):
+                raw[(k, g)] = rawp.tile([P, 4, H], BF16, name="raw%d_%d" % (k, g), tag="raw")
+            for c0, c1 in splits:
+                for g in range(PASSES):
+                    src = W1[k, 512 * g : 512 * g + 512, :].rearrange("(p j) w -> p j w", j=4)
+                    nc.sync.dma_start(out=raw[(k, g)][:, :, c0:c1], in_=src[:, :, c0:c1])
+
+        load_w(0, HEAD0_SPLITS)
+        load_w(1, [(0, H)])
+        load_w(2, [(0, H)])
+
+        wg, wc, ws, acc, gel, tps, otile = {}, {}, {}, {}, {}, {}, {}
+
+        def regroup(r):
+            k, n = divmod(r, ROUNDS_PER_HEAD)
+            wg[r] = wgp.tile([P, PASSES, NBLK, 4], BF16, name="wg%d" % r, tag="wg", align_bytes=64)
+            s = S_COLS[r]
+            for g in range(PASSES):
+                vend = NBLK - s if g == 1 else NBLK
+                if vend > 0:
+                    nc.vector.tensor_copy(
+                        out=wg[r][:, g, 0:vend, :].rearrange("p (c i) t -> p c t i", i=4),
+                        in_=raw[(k, g)][:, :, NBLK * n : NBLK * n + vend].rearrange("p t (c i) -> p c t i", i=4),
+                    )
+                if vend < NBLK:
+                    nc.scalar.copy(
+                        out=wg[r][:, g, vend:NBLK, :].rearrange("p (c i) t -> p c t i", i=4),
+                        in_=raw[(k, g)][:, :, NBLK * n + vend : NBLK * n + NBLK].rearrange("p t (c i) -> p c t i", i=4),
+                    )
+
+        def quant(r):
+            wc[r] = wcp.tile([P, PASSES * NBLK], U32, name="wc%d" % r, tag="wc", align_bytes=64)
+            ws[r] = wcp.tile([P, PASSES * NBLK], U8, name="ws%d" % r, tag="ws", align_bytes=64)
+            nc.vector.quantize_mx(
+                out=wc[r][:].bitcast(FP8X4),
+                scales=ws[r][:],
+                in_=wg[r][:].rearrange("p g c t -> p (g c t)"),
+            )
+
+        def mx(r):
+            k = r // ROUNDS_PER_HEAD
+            acc[r] = [psa.tile([P, 2, TOK], F32, name="acc%d_%d" % (r, a), tag="A") for a in range(2)]
+            for ht in range(4):
+                for g in range(PASSES):
+                    cols = slice(g * NBLK + ht * P, g * NBLK + ht * P + P)
+                    toks = slice(g * TOK, g * TOK + TOK)
+                    nc.tensor.matmul_mx(
+                        out=acc[r][ht // 2][:, ht % 2, :],
+                        lhsT=wc[r][:, cols].bitcast(FP8X4),
+                        lhsT_scale=ws[r][:, cols],
+                        rhs=yc[:, k, toks].bitcast(FP8X4),
+                        rhs_scale=ys[:, k, toks],
+                        start=(g == 0),
+                        stop=(g == PASSES - 1),
+                    )
+
+        def gelu(r):
+            gel[r] = gp.tile([P, 4, TOK], F32, name="gel%d" % r, tag="G")
+            for ht in range(4):
+                nc.scalar.activation(
+                    out=gel[r][:, ht, :],
+                    in_=acc[r][ht // 2][:, ht % 2, :],
+                    func=ACT.Gelu,
+                    bias=b1f[:, 4 * r + ht : 4 * r + ht + 1],
+                    scale=1.0,
+                )
+
+        def back(r):
+            tps[r] = [pst.tile([P, NBLK], F32, name="tp%d_%d" % (r, m), tag="T") for m in range(2)]
+            for m in range(2):
+                for ht in range(4):
+                    nc.tensor.transpose(
+                        out=tps[r][m][:, ht * P : ht * P + P],
+                        in_=gel[r][:, ht, m * P : m * P + P],
+                        identity=ident[:],
+                    )
+
+        def leave(r):
+            k, n = divmod(r, ROUNDS_PER_HEAD)
+            half, part = divmod(n, 2)
+            if part == 0:
+                otile[(k, half)] = [
+                    op.tile([P, 2 * NBLK], F32, name="o%d_%d_%d" % (k, half, m), tag="O") for m in range(2)
+                ]
+            for m in range(2):
+                dst = otile[(k, half)][m][:, part * NBLK : part * NBLK + NBLK]
+                if r >= V_OUT_FROM and m == 0:
+                    nc.vector.tensor_copy(out=dst, in_=tps[r][m][:])
+                else:
+                    nc.scalar.copy(out=dst, in_=tps[r][m][:])
+            if r >= V_OUT_FROM:
+                c0, c1 = part * NBLK, part * NBLK + NBLK
+            elif part == 1:
+                c0, c1 = 0, 2 * NBLK
+            else:
+                return
+            for m in range(2):
+                for e in range(2):
+                    nc.sync.dma_start(
+                        out=out[2 * m + e, k, :, 2 * NBLK * half + c0 : 2 * NBLK * half + c1],
+                        in_=otile[(k, half)][m][e:P:2, c0:c1],
+                    )
+
+        regroup(0)
+        regroup(1)
+
+        prmp = const.tile([P, 4, P], BF16, name="prmp")
+        nc.vector.tensor_copy(out=prmp[:], in_=prm[:, 0:512].rearrange("p (i t) -> p t i", t=4))
+        pp = psa.tile([P, 5, P], BF16, name="pp", tag="A")
+        for t in range(4):
+            nc.tensor.transpose(out=pp[:, t, :], in_=prmp[:, t, :], identity=identb[:])
+        nc.tensor.transpose(out=pp[:, 4, :], in_=prm[:, 512:640], identity=identb[:])
+        lnf = const.tile([P, 4, 16], F32, name="lnf")
+        nc.vector.tensor_copy(out=lnf[:], in_=pp[:, 0:4, 0:16])
+        b1f = const.tile([P, 64], F32, name="b1f")
+        nc.vector.tensor_copy(out=b1f[:], in_=pp[:, 4, 0:64])
+
+        st = const.tile([P, 2, 2, 6], F32, name="st")
+        mv = const.tile([P, 2, 2], F32, name="mv")
+        for m in range(2):
+            for h in range(2):
+                nc.vector.bn_stats(out=st[:, m, h, :], in_=xt[:, m, 512 * h : 512 * h + 512])
+            nc.vector.bn_aggr(out=mv[:, m, :], in_=st[:, m, :, :].rearrange("p a b -> p (a b)"))
+        ve = const.tile([P, 2], F32, name="ve")
+        nc.vector.tensor_scalar(out=ve[:], in0=mv[:, :, 1], scalar1=LN_EPS, scalar2=None, op0=ALU.add)
+        rstd = const.tile([P, 2], F32, name="rstd")
+        nc.gpsimd.tensor_tensor(out=rstd[:], in0=ve[:], in1=neghalf[:], op=ALU.pow)
+        xnp = const.tile([P, 2, PASSES, 4, P], F32, name="xnp")
+        for m in range(2):
+            nc.vector.tensor_scalar(
+                out=xnp[:, m],
+                in0=xt[:, m, :].rearrange("p (g i t) -> p g t i", g=PASSES, t=4),
+                scalar1=mv[:, m, 0:1],
+                scalar2=rstd[:, m : m + 1],
+                op0=ALU.subtract,
+                op1=ALU.mult,
+            )
+        xtb = {}
+        for g in range(PASSES):
+            for tp in range(2):
+                xtb[(g, tp)] = pst.tile([P, 2, TOK], F32, name="xtb%d_%d" % (g, tp), tag="T")
+                for t2 in range(2):
+                    for m in range(2):
+                        nc.tensor.transpose(
+                            out=xtb[(g, tp)][:, t2, m * P : m * P + P],
+                            in_=xnp[:, m, g, 2 * tp + t2, :],
+                            identity=ident[:],
+                        )
+
+        yc = const.tile([P, HEADS, PASSES * TOK], U32, name="yc", align_bytes=64)
+        ys = const.tile([P, HEADS, PASSES * TOK], U8, name="ys", align_bytes=64)
+        for k in range(HEADS):
+            ya = yp.tile([P, PASSES, 4, TOK], BF16, name="ya%d" % k, tag="ya")
+            for g in range(PASSES):
+                for t in range(4):
+                    nc.scalar.activation(
+                        out=ya[:, g, t, :],
+                        in_=xtb[(g, t // 2)][:, t % 2, :],
+                        func=ACT.Identity,
+                        scale=lnf[:, t, 2 * k + g : 2 * k + g + 1],
+                        bias=lnf[:, t, 8 + 2 * k + g : 8 + 2 * k + g + 1],
+                    )
+            yg = yp.tile([P, PASSES, TOK, 4], BF16, name="yg%d" % k, tag="yg", align_bytes=64)
+            for g in range(PASSES):
+                nc.vector.tensor_copy(
+                    out=yg[:, g].rearrange("p (c i) t -> p c t i", i=4),
+                    in_=ya[:, g].rearrange("p t (c i) -> p c t i", i=4),
+                )
+            if k == 0:
+                quant(0)
+            nc.vector.quantize_mx(
+                out=yc[:, k, :].bitcast(FP8X4),
+                scales=ys[:, k, :],
+                in_=yg[:].rearrange("p g c t -> p (g c t)"),
+            )
+
+        for i in range(ROUNDS + 2):
+            if 0 <= i - 2:
+                leave(i - 2)
+            if i + 2 < ROUNDS:
+                regroup(i + 2)
+                if i + 2 == ROUNDS_PER_HEAD - 1:
+                    load_w(3, [(0, H)])
+            if i + 1 < ROUNDS:
+                quant(i + 1)
+            if i < ROUNDS:
+                mx(i)
+            if 0 <= i - 1 < ROUNDS:
+                back(i - 1)
+            if i < ROUNDS:
+                gelu(i)

@@ -23,9 +23,13 @@ TOK = BATCH * T
 
 FLOPS = 2 * TOK * D * H * HEADS
 
-S_COLS = [512, 512, 256] + [128] * 11 + [64, 0]
-V_OUT_FROM = 14
-RAW_BUFS = 6
+PINNED = True
+S_COLS = [0, 320, 128, 384, 448, 448, 192, 128, 128, 128, 128, 128, 64, 64, 0, 0]
+V_OUT_ONE = 12
+V_OUT_BOTH = 14
+FINE_STORE = 14
+LEAD_R = 5
+LEAD_Q = 4
 HEAD0_SPLITS = [(0, 512), (512, 1024), (1024, 2048)]
 
 
@@ -33,34 +37,35 @@ def tile_twostepvoicecraftheads_pa_kernel(tc, x, ln_scale, ln_bias, W1, b1, out)
     nc = tc.nc
     with ExitStack() as ctx:
         const = ctx.enter_context(tc.tile_pool(name="const", bufs=1))
-        rawp = ctx.enter_context(tc.tile_pool(name="rawp", bufs=RAW_BUFS))
+        rawp = ctx.enter_context(tc.tile_pool(name="rawp", bufs=6))
         wgp = ctx.enter_context(tc.tile_pool(name="wgp", bufs=3))
-        wcp = ctx.enter_context(tc.tile_pool(name="wcp", bufs=4))
+        wcp = ctx.enter_context(tc.tile_pool(name="wcp", bufs=5))
         yp = ctx.enter_context(tc.tile_pool(name="yp", bufs=2))
         gp = ctx.enter_context(tc.tile_pool(name="gp", bufs=3))
-        op = ctx.enter_context(tc.tile_pool(name="op", bufs=5))
+        op = ctx.enter_context(tc.tile_pool(name="op", bufs=6))
         psa = ctx.enter_context(tc.psum_pool(name="psa", bufs=4))
         pst = ctx.enter_context(tc.psum_pool(name="pst", bufs=4))
+        if PINNED:
+            ctx.enter_context(tc.manual_schedule())
 
         ident = const.tile([P, P], F32, name="ident")
         make_identity(nc, ident[:])
+        prm = const.tile([P, 640], BF16, name="prm")
+        nc.vector.memset(prm[:].bitcast(I32), 0)
         identb = const.tile([P, P], BF16, name="identb")
         nc.vector.tensor_copy(out=identb[:], in_=ident[:])
         neghalf = const.tile([P, 2], F32, name="neghalf")
         nc.vector.memset(neghalf[:], -0.5)
         warm = const.tile([P, 1], F32, name="warm")
         nc.vector.memset(warm[:], 0.0)
-        prm = const.tile([P, 640], BF16, name="prm")
-        nc.vector.memset(prm[:].bitcast(I32), 0)
 
         xt = const.tile([P, 2, D], BF16, name="xt")
-        xv = x.rearrange("(m e) t d -> e t m d", e=2)
-        for e in range(2):
-            nc.sync.dma_start(out=xt[e:P:2, :, :], in_=xv[e])
+        for m in range(2):
+            for e in range(2):
+                nc.sync.dma_start(out=xt[e:P:2, m, :], in_=x[2 * m + e])
         nc.scalar.dma_start(out=prm[0:8, 0:512], in_=ln_scale.rearrange("k (g c) -> (k g) c", g=2))
         nc.scalar.dma_start(out=prm[8:16, 0:512], in_=ln_bias.rearrange("k (g c) -> (k g) c", g=2))
         nc.scalar.dma_start(out=prm[0:64, 512:640], in_=b1.rearrange("k (a j) -> (k a) j", j=P))
-
         warm2 = const.tile([P, 1], F32, name="warm2")
         nc.scalar.activation(out=warm2[:], in_=warm[:], func=ACT.Gelu)
 
@@ -80,22 +85,28 @@ def tile_twostepvoicecraftheads_pa_kernel(tc, x, ln_scale, ln_bias, W1, b1, out)
 
         wg, wc, ws, acc, gel, tps, otile = {}, {}, {}, {}, {}, {}, {}
 
-        def regroup(r):
+        def wg_tile(r):
+            if r not in wg:
+                wg[r] = wgp.tile([P, PASSES, NBLK, 4], BF16, name="wg%d" % r, tag="wg", align_bytes=64)
+            return wg[r]
+
+        def regroup_piece(copy, r, g, c0, c1):
             k, n = divmod(r, ROUNDS_PER_HEAD)
-            wg[r] = wgp.tile([P, PASSES, NBLK, 4], BF16, name="wg%d" % r, tag="wg", align_bytes=64)
-            s = S_COLS[r]
-            for g in range(PASSES):
-                vend = NBLK - s if g == 1 else NBLK
-                if vend > 0:
-                    nc.vector.tensor_copy(
-                        out=wg[r][:, g, 0:vend, :].rearrange("p (c i) t -> p c t i", i=4),
-                        in_=raw[(k, g)][:, :, NBLK * n : NBLK * n + vend].rearrange("p t (c i) -> p c t i", i=4),
-                    )
-                if vend < NBLK:
-                    nc.scalar.copy(
-                        out=wg[r][:, g, vend:NBLK, :].rearrange("p (c i) t -> p c t i", i=4),
-                        in_=raw[(k, g)][:, :, NBLK * n + vend : NBLK * n + NBLK].rearrange("p t (c i) -> p c t i", i=4),
-                    )
+            copy(
+                out=wg_tile(r)[:, g, c0:c1, :].rearrange("p (c i) t -> p c t i", i=4),
+                in_=raw[(k, g)][:, :, NBLK * n + c0 : NBLK * n + c1].rearrange("p t (c i) -> p c t i", i=4),
+            )
+
+        def regroup_s(r):
+            if r == 0:
+                regroup_piece(nc.scalar.copy, r, 0, 0, NBLK)
+            elif S_COLS[r] > 0:
+                regroup_piece(nc.scalar.copy, r, 1, NBLK - S_COLS[r], NBLK)
+
+        def regroup_v(r):
+            if r > 0:
+                regroup_piece(nc.vector.tensor_copy, r, 0, 0, NBLK)
+            regroup_piece(nc.vector.tensor_copy, r, 1, 0, NBLK - S_COLS[r])
 
         def quant(r):
             wc[r] = wcp.tile([P, PASSES * NBLK], U32, name="wc%d" % r, tag="wc", align_bytes=64)
@@ -136,8 +147,8 @@ def tile_twostepvoicecraftheads_pa_kernel(tc, x, ln_scale, ln_bias, W1, b1, out)
 
         def back(r):
             tps[r] = [pst.tile([P, NBLK], F32, name="tp%d_%d" % (r, m), tag="T") for m in range(2)]
-            for m in range(2):
-                for ht in range(4):
+            for ht in range(4):
+                for m in range(2):
                     nc.tensor.transpose(
                         out=tps[r][m][:, ht * P : ht * P + P],
                         in_=gel[r][:, ht, m * P : m * P + P],
@@ -153,11 +164,11 @@ def tile_twostepvoicecraftheads_pa_kernel(tc, x, ln_scale, ln_bias, W1, b1, out)
                 ]
             for m in range(2):
                 dst = otile[(k, half)][m][:, part * NBLK : part * NBLK + NBLK]
-                if r >= V_OUT_FROM and m == 0:
+                if r >= V_OUT_BOTH or (r >= V_OUT_ONE and m == 0):
                     nc.vector.tensor_copy(out=dst, in_=tps[r][m][:])
                 else:
                     nc.scalar.copy(out=dst, in_=tps[r][m][:])
-            if r >= V_OUT_FROM:
+            if r >= FINE_STORE:
                 c0, c1 = part * NBLK, part * NBLK + NBLK
             elif part == 1:
                 c0, c1 = 0, 2 * NBLK
@@ -170,20 +181,6 @@ def tile_twostepvoicecraftheads_pa_kernel(tc, x, ln_scale, ln_bias, W1, b1, out)
                         in_=otile[(k, half)][m][e:P:2, c0:c1],
                     )
 
-        regroup(0)
-        regroup(1)
-
-        prmp = const.tile([P, 4, P], BF16, name="prmp")
-        nc.vector.tensor_copy(out=prmp[:], in_=prm[:, 0:512].rearrange("p (i t) -> p t i", t=4))
-        pp = psa.tile([P, 5, P], BF16, name="pp", tag="A")
-        for t in range(4):
-            nc.tensor.transpose(out=pp[:, t, :], in_=prmp[:, t, :], identity=identb[:])
-        nc.tensor.transpose(out=pp[:, 4, :], in_=prm[:, 512:640], identity=identb[:])
-        lnf = const.tile([P, 4, 16], F32, name="lnf")
-        nc.vector.tensor_copy(out=lnf[:], in_=pp[:, 0:4, 0:16])
-        b1f = const.tile([P, 64], F32, name="b1f")
-        nc.vector.tensor_copy(out=b1f[:], in_=pp[:, 4, 0:64])
-
         st = const.tile([P, 2, 2, 6], F32, name="st")
         mv = const.tile([P, 2, 2], F32, name="mv")
         for m in range(2):
@@ -192,69 +189,130 @@ def tile_twostepvoicecraftheads_pa_kernel(tc, x, ln_scale, ln_bias, W1, b1, out)
             nc.vector.bn_aggr(out=mv[:, m, :], in_=st[:, m, :, :].rearrange("p a b -> p (a b)"))
         ve = const.tile([P, 2], F32, name="ve")
         nc.vector.tensor_scalar(out=ve[:], in0=mv[:, :, 1], scalar1=LN_EPS, scalar2=None, op0=ALU.add)
+        negmean = const.tile([P, 2], F32, name="negmean")
+        nc.vector.tensor_scalar(out=negmean[:], in0=mv[:, :, 0], scalar1=-1.0, scalar2=None, op0=ALU.mult)
         rstd = const.tile([P, 2], F32, name="rstd")
         nc.gpsimd.tensor_tensor(out=rstd[:], in0=ve[:], in1=neghalf[:], op=ALU.pow)
+        nmr = const.tile([P, 2], F32, name="nmr")
+        nc.gpsimd.tensor_tensor(out=nmr[:], in0=negmean[:], in1=rstd[:], op=ALU.mult)
+
+        prmp = const.tile([P, 4, P], BF16, name="prmp")
+        nc.vector.tensor_copy(out=prmp[:], in_=prm[:, 0:512].rearrange("p (i t) -> p t i", t=4))
+        pp = psa.tile([P, 5, P], BF16, name="pp", tag="A")
+        for t in range(4):
+            nc.tensor.transpose(out=pp[:, t, :], in_=prmp[:, t, :], identity=identb[:])
+        nc.tensor.transpose(out=pp[:, 4, :], in_=prm[:, 512:640], identity=identb[:])
+
+        regroup_s(0)
+        regroup_v(0)
+
+        lnf = const.tile([P, 4, 16], F32, name="lnf")
+        nc.vector.tensor_copy(out=lnf[:], in_=pp[:, 0:4, 0:16])
+        b1f = const.tile([P, 64], F32, name="b1f")
+        nc.vector.tensor_copy(out=b1f[:], in_=pp[:, 4, 0:64])
+
         xnp = const.tile([P, 2, PASSES, 4, P], F32, name="xnp")
-        for m in range(2):
-            nc.vector.tensor_scalar(
-                out=xnp[:, m],
-                in0=xt[:, m, :].rearrange("p (g i t) -> p g t i", g=PASSES, t=4),
-                scalar1=mv[:, m, 0:1],
-                scalar2=rstd[:, m : m + 1],
-                op0=ALU.subtract,
-                op1=ALU.mult,
-            )
+        for g in range(PASSES):
+            for m in range(2):
+                nc.scalar.activation(
+                    out=xnp[:, m, g],
+                    in_=xt[:, m, 512 * g : 512 * g + 512].rearrange("p (i t) -> p t i", t=4),
+                    func=ACT.Identity,
+                    scale=rstd[:, m : m + 1],
+                    bias=nmr[:, m : m + 1],
+                )
         xtb = {}
         for g in range(PASSES):
             for tp in range(2):
                 xtb[(g, tp)] = pst.tile([P, 2, TOK], F32, name="xtb%d_%d" % (g, tp), tag="T")
-                for t2 in range(2):
-                    for m in range(2):
-                        nc.tensor.transpose(
-                            out=xtb[(g, tp)][:, t2, m * P : m * P + P],
-                            in_=xnp[:, m, g, 2 * tp + t2, :],
-                            identity=ident[:],
-                        )
+        for g in range(PASSES):
+            for t in range(4):
+                for m in range(2):
+                    nc.tensor.transpose(
+                        out=xtb[(g, t // 2)][:, t % 2, m * P : m * P + P],
+                        in_=xnp[:, m, g, t, :],
+                        identity=ident[:],
+                    )
 
         yc = const.tile([P, HEADS, PASSES * TOK], U32, name="yc", align_bytes=64)
         ys = const.tile([P, HEADS, PASSES * TOK], U8, name="ys", align_bytes=64)
-        for k in range(HEADS):
-            ya = yp.tile([P, PASSES, 4, TOK], BF16, name="ya%d" % k, tag="ya")
+        ya, yg = {}, {}
+
+        def affine(k):
+            ya[k] = yp.tile([P, PASSES, 4, TOK], BF16, name="ya%d" % k, tag="ya")
             for g in range(PASSES):
                 for t in range(4):
                     nc.scalar.activation(
-                        out=ya[:, g, t, :],
+                        out=ya[k][:, g, t, :],
                         in_=xtb[(g, t // 2)][:, t % 2, :],
                         func=ACT.Identity,
                         scale=lnf[:, t, 2 * k + g : 2 * k + g + 1],
                         bias=lnf[:, t, 8 + 2 * k + g : 8 + 2 * k + g + 1],
                     )
-            yg = yp.tile([P, PASSES, TOK, 4], BF16, name="yg%d" % k, tag="yg", align_bytes=64)
+
+        def y_regroup(k):
+            yg[k] = yp.tile([P, PASSES, TOK, 4], BF16, name="yg%d" % k, tag="yg", align_bytes=64)
             for g in range(PASSES):
                 nc.vector.tensor_copy(
-                    out=yg[:, g].rearrange("p (c i) t -> p c t i", i=4),
-                    in_=ya[:, g].rearrange("p t (c i) -> p c t i", i=4),
+                    out=yg[k][:, g].rearrange("p (c i) t -> p c t i", i=4),
+                    in_=ya[k][:, g].rearrange("p t (c i) -> p c t i", i=4),
                 )
-            if k == 0:
-                quant(0)
+
+        def y_quant(k):
             nc.vector.quantize_mx(
                 out=yc[:, k, :].bitcast(FP8X4),
                 scales=ys[:, k, :],
-                in_=yg[:].rearrange("p g c t -> p (g c t)"),
+                in_=yg[k][:].rearrange("p g c t -> p (g c t)"),
             )
 
-        for i in range(ROUNDS + 2):
-            if 0 <= i - 2:
-                leave(i - 2)
-            if i + 2 < ROUNDS:
-                regroup(i + 2)
-                if i + 2 == ROUNDS_PER_HEAD - 1:
-                    load_w(3, [(0, H)])
-            if i + 1 < ROUNDS:
-                quant(i + 1)
-            if i < ROUNDS:
-                mx(i)
-            if 0 <= i - 1 < ROUNDS:
+        regroup_s(1)
+        regroup_v(1)
+        quant(0)
+        affine(0)
+        regroup_s(2)
+        regroup_v(2)
+        quant(1)
+        y_regroup(0)
+        affine(1)
+        regroup_s(3)
+        regroup_v(3)
+        load_w(3, [(0, H)])
+        y_quant(0)
+        mx(0)
+        quant(2)
+        y_regroup(1)
+        affine(2)
+        regroup_s(4)
+        regroup_v(4)
+        y_quant(1)
+        quant(3)
+        y_regroup(2)
+        affine(3)
+        regroup_s(5)
+        regroup_v(5)
+        y_quant(2)
+        quant(4)
+        y_regroup(3)
+        regroup_s(6)
+        regroup_v(6)
+        y_quant(3)
+        next_s, next_v, next_q = 7, 7, 5
+
+        for i in range(ROUNDS + 1):
+            if i >= 1:
                 back(i - 1)
+            if i + 1 < ROUNDS:
+                mx(i + 1)
+            while next_s < ROUNDS and next_s <= i + LEAD_R:
+                regroup_s(next_s)
+                next_s += 1
+            while next_v < ROUNDS and next_v <= i + LEAD_R:
+                regroup_v(next_v)
+                next_v += 1
+            while next_q < ROUNDS and next_q <= i + LEAD_Q:
+                quant(next_q)
+                next_q += 1
             if i < ROUNDS:
                 gelu(i)
+            if i >= 1:
+                leave(i - 1)

@@ -13,306 +13,276 @@ ACT = mybir.ActivationFunctionType
 ALU = mybir.AluOpType
 
 P = 128
+PACK = 4
+K_PASS = P * PACK
 HEADS, D, H, BATCH, T = 4, 1024, 2048, 4, 64
 LN_EPS = 1e-5
-PASSES = 2
-NBLK = 512
-ROUNDS_PER_HEAD = H // NBLK
-ROUNDS = HEADS * ROUNDS_PER_HEAD
+PASSES = D // K_PASS
 TOK = BATCH * T
+TOK_TILES = TOK // P
+COLS = 512
+H_TILES = COLS // P
+ROUNDS_PER_HEAD = H // COLS
+ROUNDS = HEADS * ROUNDS_PER_HEAD
 
 FLOPS = 2 * TOK * D * H * HEADS
 
-PINNED = True
-S_COLS = [0, 320, 128, 384, 448, 448, 192, 128, 128, 128, 128, 128, 64, 64, 0, 0]
-V_OUT_ONE = 12
-V_OUT_BOTH = 14
-FINE_STORE = 14
-LEAD_R = 5
-LEAD_Q = 4
-HEAD0_SPLITS = [(0, 512), (512, 1024), (1024, 2048)]
+SCALAR_EVERY = 3
+SCALAR_LAST = 11
+VECTOR_ONE_COPY_FROM = ROUNDS - 4
+VECTOR_BOTH_COPIES_FROM = ROUNDS - 2
+PROLOGUE_REGROUPED = HEADS + 3
+PROLOGUE_QUANTISED = HEADS + 1
+LEAD = 5
 
 
 def tile_twostepvoicecraftheads_pa_kernel(tc, x, ln_scale, ln_bias, W1, b1, out):
     nc = tc.nc
     with ExitStack() as ctx:
         const = ctx.enter_context(tc.tile_pool(name="const", bufs=1))
-        rawp = ctx.enter_context(tc.tile_pool(name="rawp", bufs=6))
-        wgp = ctx.enter_context(tc.tile_pool(name="wgp", bufs=3))
-        wcp = ctx.enter_context(tc.tile_pool(name="wcp", bufs=5))
-        yp = ctx.enter_context(tc.tile_pool(name="yp", bufs=2))
-        gp = ctx.enter_context(tc.tile_pool(name="gp", bufs=3))
-        op = ctx.enter_context(tc.tile_pool(name="op", bufs=6))
-        psa = ctx.enter_context(tc.psum_pool(name="psa", bufs=4))
-        pst = ctx.enter_context(tc.psum_pool(name="pst", bufs=4))
-        if PINNED:
-            ctx.enter_context(tc.manual_schedule())
+        raw_pool = ctx.enter_context(tc.tile_pool(name="raw", bufs=6))
+        grouped_pool = ctx.enter_context(tc.tile_pool(name="grouped", bufs=3))
+        words_pool = ctx.enter_context(tc.tile_pool(name="words", bufs=PROLOGUE_QUANTISED))
+        y_pool = ctx.enter_context(tc.tile_pool(name="y", bufs=2))
+        gelu_pool = ctx.enter_context(tc.tile_pool(name="gelu", bufs=3))
+        out_pool = ctx.enter_context(tc.tile_pool(name="outp", bufs=6))
+        sum_pool = ctx.enter_context(tc.psum_pool(name="sums", bufs=4))
+        turn_pool = ctx.enter_context(tc.psum_pool(name="turned", bufs=4))
+        ctx.enter_context(tc.manual_schedule())
 
         ident = const.tile([P, P], F32, name="ident")
         make_identity(nc, ident[:])
-        prm = const.tile([P, 640], BF16, name="prm")
-        nc.vector.memset(prm[:].bitcast(I32), 0)
-        identb = const.tile([P, P], BF16, name="identb")
-        nc.vector.tensor_copy(out=identb[:], in_=ident[:])
-        neghalf = const.tile([P, 2], F32, name="neghalf")
-        nc.vector.memset(neghalf[:], -0.5)
-        warm = const.tile([P, 1], F32, name="warm")
-        nc.vector.memset(warm[:], 0.0)
+        params = const.tile([P, K_PASS + P], BF16, name="params")
+        nc.vector.memset(params[:].bitcast(I32), 0)
+        ident_bf = const.tile([P, P], BF16, name="ident_bf")
+        nc.vector.tensor_copy(out=ident_bf[:], in_=ident[:])
+        minus_half = const.tile([P, TOK_TILES], F32, name="minus_half")
+        nc.vector.memset(minus_half[:], -0.5)
+        zero = const.tile([P, 1], F32, name="zero")
+        nc.vector.memset(zero[:], 0.0)
 
-        xt = const.tile([P, 2, D], BF16, name="xt")
-        for m in range(2):
+        x_sb = const.tile([P, TOK_TILES, D], BF16, name="x_sb")
+        for m in range(TOK_TILES):
             for e in range(2):
-                nc.sync.dma_start(out=xt[e:P:2, m, :], in_=x[2 * m + e])
-        nc.scalar.dma_start(out=prm[0:8, 0:512], in_=ln_scale.rearrange("k (g c) -> (k g) c", g=2))
-        nc.scalar.dma_start(out=prm[8:16, 0:512], in_=ln_bias.rearrange("k (g c) -> (k g) c", g=2))
-        nc.scalar.dma_start(out=prm[0:64, 512:640], in_=b1.rearrange("k (a j) -> (k a) j", j=P))
-        warm2 = const.tile([P, 1], F32, name="warm2")
-        nc.scalar.activation(out=warm2[:], in_=warm[:], func=ACT.Gelu)
+                nc.sync.dma_start(out=x_sb[e:P:2, m, :], in_=x[2 * m + e])
+        nc.scalar.dma_start(out=params[0:8, 0:K_PASS], in_=ln_scale.rearrange("k (g c) -> (k g) c", g=PASSES))
+        nc.scalar.dma_start(out=params[8:16, 0:K_PASS], in_=ln_bias.rearrange("k (g c) -> (k g) c", g=PASSES))
+        nc.scalar.dma_start(out=params[0:64, K_PASS:], in_=b1.rearrange("k (a j) -> (k a) j", j=P))
+        scratch = const.tile([P, 1], F32, name="scratch")
+        nc.scalar.activation(out=scratch[:], in_=zero[:], func=ACT.Gelu)
 
         raw = {}
 
-        def load_w(k, splits):
+        def load_w(k, col_ranges):
             for g in range(PASSES):
-                raw[(k, g)] = rawp.tile([P, 4, H], BF16, name="raw%d_%d" % (k, g), tag="raw")
-            for c0, c1 in splits:
+                raw[(k, g)] = raw_pool.tile([P, PACK, H], BF16, name="raw%d_%d" % (k, g), tag="raw")
+            for c0, c1 in col_ranges:
                 for g in range(PASSES):
-                    src = W1[k, 512 * g : 512 * g + 512, :].rearrange("(p j) w -> p j w", j=4)
-                    nc.sync.dma_start(out=raw[(k, g)][:, :, c0:c1], in_=src[:, :, c0:c1])
+                    rows = W1[k, K_PASS * g : K_PASS * (g + 1), :].rearrange("(p t) h -> p t h", t=PACK)
+                    nc.sync.dma_start(out=raw[(k, g)][:, :, c0:c1], in_=rows[:, :, c0:c1])
 
-        load_w(0, HEAD0_SPLITS)
+        load_w(0, [(0, COLS), (COLS, 2 * COLS), (2 * COLS, H)])
         load_w(1, [(0, H)])
         load_w(2, [(0, H)])
 
-        wg, wc, ws, acc, gel, tps, otile = {}, {}, {}, {}, {}, {}, {}
+        grouped, words, scales, sums, gelus, turned, out_sb = {}, {}, {}, {}, {}, {}, {}
 
-        def wg_tile(r):
-            if r not in wg:
-                wg[r] = wgp.tile([P, PASSES, NBLK, 4], BF16, name="wg%d" % r, tag="wg", align_bytes=64)
-            return wg[r]
-
-        def regroup_piece(copy, r, g, c0, c1):
-            k, n = divmod(r, ROUNDS_PER_HEAD)
-            copy(
-                out=wg_tile(r)[:, g, c0:c1, :].rearrange("p (c i) t -> p c t i", i=4),
-                in_=raw[(k, g)][:, :, NBLK * n + c0 : NBLK * n + c1].rearrange("p t (c i) -> p c t i", i=4),
-            )
-
-        def regroup_s(r):
+        def scalar_pass(r):
             if r == 0:
-                regroup_piece(nc.scalar.copy, r, 0, 0, NBLK)
-            elif S_COLS[r] > 0:
-                regroup_piece(nc.scalar.copy, r, 1, NBLK - S_COLS[r], NBLK)
+                return 0
+            if r % SCALAR_EVERY == SCALAR_EVERY - 1 and r <= SCALAR_LAST:
+                return 1
+            return None
 
-        def regroup_v(r):
-            if r > 0:
-                regroup_piece(nc.vector.tensor_copy, r, 0, 0, NBLK)
-            regroup_piece(nc.vector.tensor_copy, r, 1, 0, NBLK - S_COLS[r])
+        def regroup(r):
+            k, n = divmod(r, ROUNDS_PER_HEAD)
+            grouped[r] = grouped_pool.tile([P, PASSES, COLS, PACK], BF16, name="grouped%d" % r, tag="grouped", align_bytes=64)
+            for g in range(PASSES):
+                copy = nc.scalar.copy if g == scalar_pass(r) else nc.vector.tensor_copy
+                copy(
+                    out=grouped[r][:, g].rearrange("p (c i) t -> p c t i", i=4),
+                    in_=raw[(k, g)][:, :, COLS * n : COLS * (n + 1)].rearrange("p t (c i) -> p c t i", i=4),
+                )
 
-        def quant(r):
-            wc[r] = wcp.tile([P, PASSES * NBLK], U32, name="wc%d" % r, tag="wc", align_bytes=64)
-            ws[r] = wcp.tile([P, PASSES * NBLK], U8, name="ws%d" % r, tag="ws", align_bytes=64)
+        def quantise(r):
+            words[r] = words_pool.tile([P, PASSES * COLS], U32, name="words%d" % r, tag="words", align_bytes=64)
+            scales[r] = words_pool.tile([P, PASSES * COLS], U8, name="scales%d" % r, tag="scales", align_bytes=64)
             nc.vector.quantize_mx(
-                out=wc[r][:].bitcast(FP8X4),
-                scales=ws[r][:],
-                in_=wg[r][:].rearrange("p g c t -> p (g c t)"),
+                out=words[r][:].bitcast(FP8X4),
+                scales=scales[r][:],
+                in_=grouped[r][:].rearrange("p g h t -> p (g h t)"),
             )
 
-        def mx(r):
+        def multiply(r):
             k = r // ROUNDS_PER_HEAD
-            acc[r] = [psa.tile([P, 2, TOK], F32, name="acc%d_%d" % (r, a), tag="A") for a in range(2)]
-            for ht in range(4):
+            sums[r] = [sum_pool.tile([P, 2, TOK], F32, name="sums%d_%d" % (r, a), tag="sums") for a in range(H_TILES // 2)]
+            for a in range(H_TILES):
                 for g in range(PASSES):
-                    cols = slice(g * NBLK + ht * P, g * NBLK + ht * P + P)
-                    toks = slice(g * TOK, g * TOK + TOK)
+                    h_cols = slice(g * COLS + a * P, g * COLS + (a + 1) * P)
+                    tokens = slice(g * TOK, (g + 1) * TOK)
                     nc.tensor.matmul_mx(
-                        out=acc[r][ht // 2][:, ht % 2, :],
-                        lhsT=wc[r][:, cols].bitcast(FP8X4),
-                        lhsT_scale=ws[r][:, cols],
-                        rhs=yc[:, k, toks].bitcast(FP8X4),
-                        rhs_scale=ys[:, k, toks],
+                        out=sums[r][a // 2][:, a % 2, :],
+                        lhsT=words[r][:, h_cols].bitcast(FP8X4),
+                        lhsT_scale=scales[r][:, h_cols],
+                        rhs=y_words[:, k, tokens].bitcast(FP8X4),
+                        rhs_scale=y_scales[:, k, tokens],
                         start=(g == 0),
                         stop=(g == PASSES - 1),
                     )
 
-        def gelu(r):
-            gel[r] = gp.tile([P, 4, TOK], F32, name="gel%d" % r, tag="G")
-            for ht in range(4):
+        def bias_gelu(r):
+            gelus[r] = gelu_pool.tile([P, H_TILES, TOK], F32, name="gelus%d" % r, tag="gelus")
+            for a in range(H_TILES):
                 nc.scalar.activation(
-                    out=gel[r][:, ht, :],
-                    in_=acc[r][ht // 2][:, ht % 2, :],
+                    out=gelus[r][:, a, :],
+                    in_=sums[r][a // 2][:, a % 2, :],
                     func=ACT.Gelu,
-                    bias=b1f[:, 4 * r + ht : 4 * r + ht + 1],
+                    bias=b1_col[:, H_TILES * r + a : H_TILES * r + a + 1],
                     scale=1.0,
                 )
 
-        def back(r):
-            tps[r] = [pst.tile([P, NBLK], F32, name="tp%d_%d" % (r, m), tag="T") for m in range(2)]
-            for ht in range(4):
-                for m in range(2):
+        def turn_back(r):
+            turned[r] = [turn_pool.tile([P, COLS], F32, name="turned%d_%d" % (r, m), tag="turned") for m in range(TOK_TILES)]
+            for a in range(H_TILES):
+                for m in range(TOK_TILES):
                     nc.tensor.transpose(
-                        out=tps[r][m][:, ht * P : ht * P + P],
-                        in_=gel[r][:, ht, m * P : m * P + P],
+                        out=turned[r][m][:, a * P : (a + 1) * P],
+                        in_=gelus[r][:, a, m * P : (m + 1) * P],
                         identity=ident[:],
                     )
 
-        def leave(r):
+        def copy_out_and_store(r):
             k, n = divmod(r, ROUNDS_PER_HEAD)
-            half, part = divmod(n, 2)
-            if part == 0:
-                otile[(k, half)] = [
-                    op.tile([P, 2 * NBLK], F32, name="o%d_%d_%d" % (k, half, m), tag="O") for m in range(2)
+            pair, second = divmod(n, 2)
+            if not second:
+                out_sb[(k, pair)] = [
+                    out_pool.tile([P, 2 * COLS], F32, name="out%d_%d_%d" % (k, pair, m), tag="out") for m in range(TOK_TILES)
                 ]
-            for m in range(2):
-                dst = otile[(k, half)][m][:, part * NBLK : part * NBLK + NBLK]
-                if r >= V_OUT_BOTH or (r >= V_OUT_ONE and m == 0):
-                    nc.vector.tensor_copy(out=dst, in_=tps[r][m][:])
-                else:
-                    nc.scalar.copy(out=dst, in_=tps[r][m][:])
-            if r >= FINE_STORE:
-                c0, c1 = part * NBLK, part * NBLK + NBLK
-            elif part == 1:
-                c0, c1 = 0, 2 * NBLK
+            for m in range(TOK_TILES):
+                on_vector = r >= VECTOR_BOTH_COPIES_FROM or (r >= VECTOR_ONE_COPY_FROM and m == 0)
+                copy = nc.vector.tensor_copy if on_vector else nc.scalar.copy
+                copy(out=out_sb[(k, pair)][m][:, second * COLS : (second + 1) * COLS], in_=turned[r][m][:])
+            if r >= ROUNDS - 2:
+                c0, c1 = second * COLS, (second + 1) * COLS
+            elif second:
+                c0, c1 = 0, 2 * COLS
             else:
                 return
-            for m in range(2):
+            for m in range(TOK_TILES):
                 for e in range(2):
                     nc.sync.dma_start(
-                        out=out[2 * m + e, k, :, 2 * NBLK * half + c0 : 2 * NBLK * half + c1],
-                        in_=otile[(k, half)][m][e:P:2, c0:c1],
+                        out=out[2 * m + e, k, :, 2 * COLS * pair + c0 : 2 * COLS * pair + c1],
+                        in_=out_sb[(k, pair)][m][e:P:2, c0:c1],
                     )
 
-        st = const.tile([P, 2, 2, 6], F32, name="st")
-        mv = const.tile([P, 2, 2], F32, name="mv")
-        for m in range(2):
-            for h in range(2):
-                nc.vector.bn_stats(out=st[:, m, h, :], in_=xt[:, m, 512 * h : 512 * h + 512])
-            nc.vector.bn_aggr(out=mv[:, m, :], in_=st[:, m, :, :].rearrange("p a b -> p (a b)"))
-        ve = const.tile([P, 2], F32, name="ve")
-        nc.vector.tensor_scalar(out=ve[:], in0=mv[:, :, 1], scalar1=LN_EPS, scalar2=None, op0=ALU.add)
-        negmean = const.tile([P, 2], F32, name="negmean")
-        nc.vector.tensor_scalar(out=negmean[:], in0=mv[:, :, 0], scalar1=-1.0, scalar2=None, op0=ALU.mult)
-        rstd = const.tile([P, 2], F32, name="rstd")
-        nc.gpsimd.tensor_tensor(out=rstd[:], in0=ve[:], in1=neghalf[:], op=ALU.pow)
-        nmr = const.tile([P, 2], F32, name="nmr")
-        nc.gpsimd.tensor_tensor(out=nmr[:], in0=negmean[:], in1=rstd[:], op=ALU.mult)
+        stats = const.tile([P, TOK_TILES, 2, 6], F32, name="stats")
+        mean_var = const.tile([P, TOK_TILES, 2], F32, name="mean_var")
+        for m in range(TOK_TILES):
+            for half in range(2):
+                nc.vector.bn_stats(out=stats[:, m, half, :], in_=x_sb[:, m, 512 * half : 512 * (half + 1)])
+            nc.vector.bn_aggr(out=mean_var[:, m, :], in_=stats[:, m, :, :].rearrange("p a b -> p (a b)"))
+        var_eps = const.tile([P, TOK_TILES], F32, name="var_eps")
+        nc.vector.tensor_scalar(out=var_eps[:], in0=mean_var[:, :, 1], scalar1=LN_EPS, scalar2=None, op0=ALU.add)
+        minus_mean = const.tile([P, TOK_TILES], F32, name="minus_mean")
+        nc.vector.tensor_scalar(out=minus_mean[:], in0=mean_var[:, :, 0], scalar1=-1.0, scalar2=None, op0=ALU.mult)
+        rstd = const.tile([P, TOK_TILES], F32, name="rstd")
+        nc.gpsimd.tensor_tensor(out=rstd[:], in0=var_eps[:], in1=minus_half[:], op=ALU.pow)
+        shift = const.tile([P, TOK_TILES], F32, name="shift")
+        nc.gpsimd.tensor_tensor(out=shift[:], in0=minus_mean[:], in1=rstd[:], op=ALU.mult)
 
-        prmp = const.tile([P, 4, P], BF16, name="prmp")
-        nc.vector.tensor_copy(out=prmp[:], in_=prm[:, 0:512].rearrange("p (i t) -> p t i", t=4))
-        pp = psa.tile([P, 5, P], BF16, name="pp", tag="A")
-        for t in range(4):
-            nc.tensor.transpose(out=pp[:, t, :], in_=prmp[:, t, :], identity=identb[:])
-        nc.tensor.transpose(out=pp[:, 4, :], in_=prm[:, 512:640], identity=identb[:])
+        params_by_t = const.tile([P, PACK, P], BF16, name="params_by_t")
+        nc.vector.tensor_copy(out=params_by_t[:], in_=params[:, 0:K_PASS].rearrange("r (p t) -> r t p", t=PACK))
+        params_ps = sum_pool.tile([P, PACK + 1, P], BF16, name="params_ps", tag="sums")
+        for t in range(PACK):
+            nc.tensor.transpose(out=params_ps[:, t, :], in_=params_by_t[:, t, :], identity=ident_bf[:])
+        nc.tensor.transpose(out=params_ps[:, PACK, :], in_=params[:, K_PASS:], identity=ident_bf[:])
 
-        regroup_s(0)
-        regroup_v(0)
+        regroup(0)
 
-        lnf = const.tile([P, 4, 16], F32, name="lnf")
-        nc.vector.tensor_copy(out=lnf[:], in_=pp[:, 0:4, 0:16])
-        b1f = const.tile([P, 64], F32, name="b1f")
-        nc.vector.tensor_copy(out=b1f[:], in_=pp[:, 4, 0:64])
+        ln_col = const.tile([P, PACK, 16], F32, name="ln_col")
+        nc.vector.tensor_copy(out=ln_col[:], in_=params_ps[:, 0:PACK, 0:16])
+        b1_col = const.tile([P, HEADS * H // P], F32, name="b1_col")
+        nc.vector.tensor_copy(out=b1_col[:], in_=params_ps[:, PACK, 0 : HEADS * H // P])
 
-        xnp = const.tile([P, 2, PASSES, 4, P], F32, name="xnp")
+        xn = const.tile([P, TOK_TILES, PASSES, PACK, P], F32, name="xn")
         for g in range(PASSES):
-            for m in range(2):
+            for m in range(TOK_TILES):
                 nc.scalar.activation(
-                    out=xnp[:, m, g],
-                    in_=xt[:, m, 512 * g : 512 * g + 512].rearrange("p (i t) -> p t i", t=4),
+                    out=xn[:, m, g],
+                    in_=x_sb[:, m, K_PASS * g : K_PASS * (g + 1)].rearrange("n (p t) -> n t p", t=PACK),
                     func=ACT.Identity,
                     scale=rstd[:, m : m + 1],
-                    bias=nmr[:, m : m + 1],
+                    bias=shift[:, m : m + 1],
                 )
-        xtb = {}
+        xn_t = {}
         for g in range(PASSES):
-            for tp in range(2):
-                xtb[(g, tp)] = pst.tile([P, 2, TOK], F32, name="xtb%d_%d" % (g, tp), tag="T")
-        for g in range(PASSES):
-            for t in range(4):
-                for m in range(2):
+            for t in range(PACK):
+                if t % 2 == 0:
+                    xn_t[(g, t // 2)] = turn_pool.tile([P, 2, TOK], F32, name="xn_t%d_%d" % (g, t // 2), tag="turned")
+                for m in range(TOK_TILES):
                     nc.tensor.transpose(
-                        out=xtb[(g, t // 2)][:, t % 2, m * P : m * P + P],
-                        in_=xnp[:, m, g, t, :],
+                        out=xn_t[(g, t // 2)][:, t % 2, m * P : (m + 1) * P],
+                        in_=xn[:, m, g, t, :],
                         identity=ident[:],
                     )
 
-        yc = const.tile([P, HEADS, PASSES * TOK], U32, name="yc", align_bytes=64)
-        ys = const.tile([P, HEADS, PASSES * TOK], U8, name="ys", align_bytes=64)
-        ya, yg = {}, {}
+        y_words = const.tile([P, HEADS, PASSES * TOK], U32, name="y_words", align_bytes=64)
+        y_scales = const.tile([P, HEADS, PASSES * TOK], U8, name="y_scales", align_bytes=64)
+        y_planes, y_grouped = {}, {}
 
         def affine(k):
-            ya[k] = yp.tile([P, PASSES, 4, TOK], BF16, name="ya%d" % k, tag="ya")
+            y_planes[k] = y_pool.tile([P, PASSES, PACK, TOK], BF16, name="y_planes%d" % k, tag="y_planes")
             for g in range(PASSES):
-                for t in range(4):
+                for t in range(PACK):
+                    row = PASSES * k + g
                     nc.scalar.activation(
-                        out=ya[k][:, g, t, :],
-                        in_=xtb[(g, t // 2)][:, t % 2, :],
+                        out=y_planes[k][:, g, t, :],
+                        in_=xn_t[(g, t // 2)][:, t % 2, :],
                         func=ACT.Identity,
-                        scale=lnf[:, t, 2 * k + g : 2 * k + g + 1],
-                        bias=lnf[:, t, 8 + 2 * k + g : 8 + 2 * k + g + 1],
+                        scale=ln_col[:, t, row : row + 1],
+                        bias=ln_col[:, t, 8 + row : 8 + row + 1],
                     )
 
         def y_regroup(k):
-            yg[k] = yp.tile([P, PASSES, TOK, 4], BF16, name="yg%d" % k, tag="yg", align_bytes=64)
+            y_grouped[k] = y_pool.tile([P, PASSES, TOK, PACK], BF16, name="y_grouped%d" % k, tag="y_grouped", align_bytes=64)
             for g in range(PASSES):
                 nc.vector.tensor_copy(
-                    out=yg[k][:, g].rearrange("p (c i) t -> p c t i", i=4),
-                    in_=ya[k][:, g].rearrange("p t (c i) -> p c t i", i=4),
+                    out=y_grouped[k][:, g].rearrange("p (c i) t -> p c t i", i=4),
+                    in_=y_planes[k][:, g].rearrange("p t (c i) -> p c t i", i=4),
                 )
 
-        def y_quant(k):
+        def y_quantise(k):
             nc.vector.quantize_mx(
-                out=yc[:, k, :].bitcast(FP8X4),
-                scales=ys[:, k, :],
-                in_=yg[k][:].rearrange("p g c t -> p (g c t)"),
+                out=y_words[:, k, :].bitcast(FP8X4),
+                scales=y_scales[:, k, :],
+                in_=y_grouped[k][:].rearrange("p g n t -> p (g n t)"),
             )
 
-        regroup_s(1)
-        regroup_v(1)
-        quant(0)
-        affine(0)
-        regroup_s(2)
-        regroup_v(2)
-        quant(1)
-        y_regroup(0)
-        affine(1)
-        regroup_s(3)
-        regroup_v(3)
-        load_w(3, [(0, H)])
-        y_quant(0)
-        mx(0)
-        quant(2)
-        y_regroup(1)
-        affine(2)
-        regroup_s(4)
-        regroup_v(4)
-        y_quant(1)
-        quant(3)
-        y_regroup(2)
-        affine(3)
-        regroup_s(5)
-        regroup_v(5)
-        y_quant(2)
-        quant(4)
-        y_regroup(3)
-        regroup_s(6)
-        regroup_v(6)
-        y_quant(3)
-        next_s, next_v, next_q = 7, 7, 5
+        regroup(1)
+        quantise(0)
+        for k in range(HEADS):
+            affine(k)
+            regroup(k + 2)
+            if k == 1:
+                load_w(3, [(0, H)])
+            if k >= 1:
+                y_quantise(k - 1)
+            quantise(k + 1)
+            y_regroup(k)
+        regroup(HEADS + 2)
+        y_quantise(HEADS - 1)
+        multiply(0)
 
         for i in range(ROUNDS + 1):
             if i >= 1:
-                back(i - 1)
+                turn_back(i - 1)
             if i + 1 < ROUNDS:
-                mx(i + 1)
-            while next_s < ROUNDS and next_s <= i + LEAD_R:
-                regroup_s(next_s)
-                next_s += 1
-            while next_v < ROUNDS and next_v <= i + LEAD_R:
-                regroup_v(next_v)
-                next_v += 1
-            while next_q < ROUNDS and next_q <= i + LEAD_Q:
-                quant(next_q)
-                next_q += 1
+                multiply(i + 1)
+            if PROLOGUE_REGROUPED <= i + LEAD < ROUNDS:
+                regroup(i + LEAD)
+            if PROLOGUE_QUANTISED <= i + LEAD - 1 < ROUNDS:
+                quantise(i + LEAD - 1)
             if i < ROUNDS:
-                gelu(i)
+                bias_gelu(i)
             if i >= 1:
-                leave(i - 1)
+                copy_out_and_store(i - 1)

@@ -27,7 +27,7 @@ ROUNDS = HEADS * ROUNDS_PER_HEAD
 
 FLOPS = 2 * TOK * D * H * HEADS
 
-SCALAR_EVERY = 3
+SCALAR_EVERY = 2
 SCALAR_LAST = 11
 VECTOR_ONE_COPY_FROM = ROUNDS - 4
 VECTOR_BOTH_COPIES_FROM = ROUNDS - 2

@@ -73,17 +73,27 @@ def tile_twostepvoicecraftheads_pa_kernel(tc, x, ln_scale, ln_bias, W1, b1, out)
 
         raw = {}
 
-        def load_w(k, col_ranges):
-            for g in range(PASSES):
-                raw[(k, g)] = raw_pool.tile([P, PACK, H], BF16, name="raw%d_%d" % (k, g), tag="raw")
-            for c0, c1 in col_ranges:
+        def load_w(k, by_round):
+            rows = [W1[k, K_PASS * g : K_PASS * (g + 1), :].rearrange("(p t) h -> p t h", t=PACK) for g in range(PASSES)]
+            if by_round:
+                tiles = [
+                    raw_pool.tile([P, ROUNDS_PER_HEAD, PACK, COLS], BF16, name="raw%d_%d" % (k, g), tag="raw")
+                    for g in range(PASSES)
+                ]
+                for n in range(ROUNDS_PER_HEAD):
+                    for g in range(PASSES):
+                        raw[(k, g, n)] = tiles[g][:, n]
+                        nc.sync.dma_start(out=raw[(k, g, n)], in_=rows[g][:, :, COLS * n : COLS * (n + 1)])
+            else:
                 for g in range(PASSES):
-                    rows = W1[k, K_PASS * g : K_PASS * (g + 1), :].rearrange("(p t) h -> p t h", t=PACK)
-                    nc.sync.dma_start(out=raw[(k, g)][:, :, c0:c1], in_=rows[:, :, c0:c1])
+                    whole = raw_pool.tile([P, PACK, H], BF16, name="raw%d_%d" % (k, g), tag="raw")
+                    nc.sync.dma_start(out=whole[:], in_=rows[g])
+                    for n in range(ROUNDS_PER_HEAD):
+                        raw[(k, g, n)] = whole[:, :, COLS * n : COLS * (n + 1)]
 
-        load_w(0, [(0, COLS), (COLS, 2 * COLS), (2 * COLS, H)])
-        load_w(1, [(0, H)])
-        load_w(2, [(0, H)])
+        load_w(0, True)
+        load_w(1, False)
+        load_w(2, False)
 
         grouped, words, scales, sums, gelus, turned, out_sb = {}, {}, {}, {}, {}, {}, {}
 
@@ -101,7 +111,7 @@ def tile_twostepvoicecraftheads_pa_kernel(tc, x, ln_scale, ln_bias, W1, b1, out)
                 copy = nc.scalar.copy if g == scalar_pass(r) else nc.vector.tensor_copy
                 copy(
                     out=grouped[r][:, g].rearrange("p (c i) t -> p c t i", i=4),
-                    in_=raw[(k, g)][:, :, COLS * n : COLS * (n + 1)].rearrange("p t (c i) -> p c t i", i=4),
+                    in_=raw[(k, g, n)].rearrange("p t (c i) -> p c t i", i=4),
                 )
 
         def quantise(r):
@@ -264,7 +274,7 @@ def tile_twostepvoicecraftheads_pa_kernel(tc, x, ln_scale, ln_bias, W1, b1, out)
             affine(k)
             regroup(k + 2)
             if k == 1:
-                load_w(3, [(0, H)])
+                load_w(3, False)
             if k >= 1:
                 y_quantise(k - 1)
             quantise(k + 1)

@@ -62,9 +62,9 @@ def tile_twostepvoicecraftheads_pa_kernel(tc, x, ln_scale, ln_bias, W1, b1, out)
         nc.vector.memset(zero[:], 0.0)
 
         x_sb = const.tile([P, TOK_TILES, D], BF16, name="x_sb")
-        for m in range(TOK_TILES):
-            for e in range(2):
-                nc.sync.dma_start(out=x_sb[e:P:2, m, :], in_=x[2 * m + e])
+        x_by_parity = x.rearrange("(m e) t d -> e t m d", e=2)
+        for e in range(2):
+            nc.sync.dma_start(out=x_sb[e:P:2, :, :], in_=x_by_parity[e])
         nc.scalar.dma_start(out=params[0:8, 0:K_PASS], in_=ln_scale.rearrange("k (g c) -> (k g) c", g=PASSES))
         nc.scalar.dma_start(out=params[8:16, 0:K_PASS], in_=ln_bias.rearrange("k (g c) -> (k g) c", g=PASSES))
         nc.scalar.dma_start(out=params[0:64, K_PASS:], in_=b1.rearrange("k (a j) -> (k a) j", j=P))
@@ -92,7 +92,7 @@ def tile_twostepvoicecraftheads_pa_kernel(tc, x, ln_scale, ln_bias, W1, b1, out)
                         raw[(k, g, n)] = whole[:, :, COLS * n : COLS * (n + 1)]
 
         load_w(0, True)
-        load_w(1, False)
+        load_w(1, True)
         load_w(2, False)
 
         grouped, words, scales, sums, gelus, turned, out_sb = {}, {}, {}, {}, {}, {}, {}

@@ -48,7 +48,6 @@ def tile_twostepvoicecraftheads_pa_kernel(tc, x, ln_scale, ln_bias, W1, b1, out)
         out_pool = ctx.enter_context(tc.tile_pool(name="outp", bufs=6))
         sum_pool = ctx.enter_context(tc.psum_pool(name="sums", bufs=4))
         turn_pool = ctx.enter_context(tc.psum_pool(name="turned", bufs=4))
-        ctx.enter_context(tc.manual_schedule())
 
         ident = const.tile([P, P], F32, name="ident")
         make_identity(nc, ident[:])
@@ -62,9 +61,9 @@ def tile_twostepvoicecraftheads_pa_kernel(tc, x, ln_scale, ln_bias, W1, b1, out)
         nc.vector.memset(zero[:], 0.0)
 
         x_sb = const.tile([P, TOK_TILES, D], BF16, name="x_sb")
-        x_by_parity = x.rearrange("(m e) t d -> e t m d", e=2)
-        for e in range(2):
-            nc.sync.dma_start(out=x_sb[e:P:2, :, :], in_=x_by_parity[e])
+        for m in range(TOK_TILES):
+            for e in range(2):
+                nc.sync.dma_start(out=x_sb[e:P:2, m, :], in_=x[2 * m + e])
         nc.scalar.dma_start(out=params[0:8, 0:K_PASS], in_=ln_scale.rearrange("k (g c) -> (k g) c", g=PASSES))
         nc.scalar.dma_start(out=params[8:16, 0:K_PASS], in_=ln_bias.rearrange("k (g c) -> (k g) c", g=PASSES))
         nc.scalar.dma_start(out=params[0:64, K_PASS:], in_=b1.rearrange("k (a j) -> (k a) j", j=P))
@@ -92,7 +91,7 @@ def tile_twostepvoicecraftheads_pa_kernel(tc, x, ln_scale, ln_bias, W1, b1, out)
                         raw[(k, g, n)] = whole[:, :, COLS * n : COLS * (n + 1)]
 
         load_w(0, True)
-        load_w(1, True)
+        load_w(1, False)
         load_w(2, False)
 
         grouped, words, scales, sums, gelus, turned, out_sb = {}, {}, {}, {}, {}, {}, {}

@@ -48,6 +48,7 @@ def tile_twostepvoicecraftheads_pa_kernel(tc, x, ln_scale, ln_bias, W1, b1, out)
         out_pool = ctx.enter_context(tc.tile_pool(name="outp", bufs=6))
         sum_pool = ctx.enter_context(tc.psum_pool(name="sums", bufs=4))
         turn_pool = ctx.enter_context(tc.psum_pool(name="turned", bufs=4))
+        ctx.enter_context(tc.manual_schedule())
 
         ident = const.tile([P, P], F32, name="ident")
         make_identity(nc, ident[:])
@@ -72,55 +73,44 @@ def tile_twostepvoicecraftheads_pa_kernel(tc, x, ln_scale, ln_bias, W1, b1, out)
 
         raw = {}
 
-        def load_w(k, by_round):
-            rows = [W1[k, K_PASS * g : K_PASS * (g + 1), :].rearrange("(p t) h -> p t h", t=PACK) for g in range(PASSES)]
-            if by_round:
-                tiles = [
-                    raw_pool.tile([P, ROUNDS_PER_HEAD, PACK, COLS], BF16, name="raw%d_%d" % (k, g), tag="raw")
-                    for g in range(PASSES)
-                ]
-                for n in range(ROUNDS_PER_HEAD):
-                    for g in range(PASSES):
-                        raw[(k, g, n)] = tiles[g][:, n]
-                        nc.sync.dma_start(out=raw[(k, g, n)], in_=rows[g][:, :, COLS * n : COLS * (n + 1)])
-            else:
-                for g in range(PASSES):
-                    whole = raw_pool.tile([P, PACK, H], BF16, name="raw%d_%d" % (k, g), tag="raw")
-                    nc.sync.dma_start(out=whole[:], in_=rows[g])
-                    for n in range(ROUNDS_PER_HEAD):
-                        raw[(k, g, n)] = whole[:, :, COLS * n : COLS * (n + 1)]
+        def load_w(k):
+            for g in range(PASSES):
+                raw[(k, g)] = raw_pool.tile([P, PACK, H], BF16, name="raw%d_%d" % (k, g), tag="raw")
+                rows = W1[k, K_PASS * g : K_PASS * (g + 1), :].rearrange("(p t) h -> p t h", t=PACK)
+                nc.sync.dma_start(out=raw[(k, g)][:], in_=rows)
 
-        load_w(0, True)
-        load_w(1, False)
-        load_w(2, False)
+        for k in range(3):
+            load_w(k)
 
         grouped, words, scales, sums, gelus, turned, out_sb = {}, {}, {}, {}, {}, {}, {}
 
-        def scalar_pass(r):
-            if r == 0:
-                return 0
-            if r % SCALAR_EVERY == SCALAR_EVERY - 1 and r <= SCALAR_LAST:
-                return 1
-            return None
+        def blocks(s):
+            if s < ROUNDS_PER_HEAD:
+                g, r = divmod(2 * s, ROUNDS_PER_HEAD)
+                return [(r, g), (r + 1, g)]
+            return [(s, 0), (s, 1)]
 
-        def regroup(r):
-            k, n = divmod(r, ROUNDS_PER_HEAD)
-            grouped[r] = grouped_pool.tile([P, PASSES, COLS, PACK], BF16, name="grouped%d" % r, tag="grouped", align_bytes=64)
-            for g in range(PASSES):
-                copy = nc.scalar.copy if g == scalar_pass(r) else nc.vector.tensor_copy
+        def regroup(s):
+            grouped[s] = grouped_pool.tile([P, 2, COLS, PACK], BF16, name="grouped%d" % s, tag="grouped", align_bytes=64)
+            for b, (r, g) in enumerate(blocks(s)):
+                k, n = divmod(r, ROUNDS_PER_HEAD)
+                on_scalar = b == 1 and s % SCALAR_EVERY == 1 and s <= SCALAR_LAST
+                copy = nc.scalar.copy if on_scalar else nc.vector.tensor_copy
                 copy(
-                    out=grouped[r][:, g].rearrange("p (c i) t -> p c t i", i=4),
-                    in_=raw[(k, g, n)].rearrange("p t (c i) -> p c t i", i=4),
+                    out=grouped[s][:, b].rearrange("p (c i) t -> p c t i", i=4),
+                    in_=raw[(k, g)][:, :, COLS * n : COLS * (n + 1)].rearrange("p t (c i) -> p c t i", i=4),
                 )
 
-        def quantise(r):
-            words[r] = words_pool.tile([P, PASSES * COLS], U32, name="words%d" % r, tag="words", align_bytes=64)
-            scales[r] = words_pool.tile([P, PASSES * COLS], U8, name="scales%d" % r, tag="scales", align_bytes=64)
-            nc.vector.quantize_mx(
-                out=words[r][:].bitcast(FP8X4),
-                scales=scales[r][:],
-                in_=grouped[r][:].rearrange("p g h t -> p (g h t)"),
-            )
+        def quantise(s):
+            for b, (r, g) in enumerate(blocks(s)):
+                if r not in words:
+                    words[r] = words_pool.tile([P, PASSES * COLS], U32, name="words%d" % r, tag="words", align_bytes=64)
+                    scales[r] = words_pool.tile([P, PASSES * COLS], U8, name="scales%d" % r, tag="scales", align_bytes=64)
+                nc.vector.quantize_mx(
+                    out=words[r][:, g * COLS : (g + 1) * COLS].bitcast(FP8X4),
+                    scales=scales[r][:, g * COLS : (g + 1) * COLS],
+                    in_=grouped[s][:, b].rearrange("p h t -> p (h t)"),
+                )
 
         def multiply(r):
             k = r // ROUNDS_PER_HEAD
@@ -273,7 +263,7 @@ def tile_twostepvoicecraftheads_pa_kernel(tc, x, ln_scale, ln_bias, W1, b1, out)
             affine(k)
             regroup(k + 2)
             if k == 1:
-                load_w(3, False)
+                load_w(3)
             if k >= 1:
                 y_quantise(k - 1)
             quantise(k + 1)

@@ -45,7 +45,7 @@ def tile_twostepvoicecraftheads_pa_kernel(tc, x, ln_scale, ln_bias, W1, b1, out)
         words_pool = ctx.enter_context(tc.tile_pool(name="words", bufs=PROLOGUE_QUANTISED))
         y_pool = ctx.enter_context(tc.tile_pool(name="y", bufs=2))
         gelu_pool = ctx.enter_context(tc.tile_pool(name="gelu", bufs=3))
-        out_pool = ctx.enter_context(tc.tile_pool(name="outp", bufs=6))
+        out_pool = ctx.enter_context(tc.tile_pool(name="outp", bufs=8))
         sum_pool = ctx.enter_context(tc.psum_pool(name="sums", bufs=4))
         turn_pool = ctx.enter_context(tc.psum_pool(name="turned", bufs=4))
         ctx.enter_context(tc.manual_schedule())

@@ -27,8 +27,9 @@ ROUNDS = HEADS * ROUNDS_PER_HEAD
 
 FLOPS = 2 * TOK * D * H * HEADS
 
-SCALAR_EVERY = 2
-SCALAR_LAST = 11
+SCALAR_STEPS = (1, 3)
+TENSOR_FROM = 4
+HALF = COLS // 2
 VECTOR_ONE_COPY_FROM = ROUNDS - 4
 VECTOR_BOTH_COPIES_FROM = ROUNDS - 2
 PROLOGUE_REGROUPED = HEADS + 3
@@ -47,7 +48,8 @@ def tile_twostepvoicecraftheads_pa_kernel(tc, x, ln_scale, ln_bias, W1, b1, out)
         gelu_pool = ctx.enter_context(tc.tile_pool(name="gelu", bufs=3))
         out_pool = ctx.enter_context(tc.tile_pool(name="outp", bufs=8))
         sum_pool = ctx.enter_context(tc.psum_pool(name="sums", bufs=4))
-        turn_pool = ctx.enter_context(tc.psum_pool(name="turned", bufs=4))
+        bank_pool = ctx.enter_context(tc.psum_pool(name="bank", bufs=1))
+        turn_pool = ctx.enter_context(tc.psum_pool(name="turned", bufs=3))
         ctx.enter_context(tc.manual_schedule())
 
         ident = const.tile([P, P], F32, name="ident")
@@ -65,9 +67,9 @@ def tile_twostepvoicecraftheads_pa_kernel(tc, x, ln_scale, ln_bias, W1, b1, out)
         for m in range(TOK_TILES):
             for e in range(2):
                 nc.sync.dma_start(out=x_sb[e:P:2, m, :], in_=x[2 * m + e])
-        nc.scalar.dma_start(out=params[0:8, 0:K_PASS], in_=ln_scale.rearrange("k (g c) -> (k g) c", g=PASSES))
-        nc.scalar.dma_start(out=params[8:16, 0:K_PASS], in_=ln_bias.rearrange("k (g c) -> (k g) c", g=PASSES))
-        nc.scalar.dma_start(out=params[0:64, K_PASS:], in_=b1.rearrange("k (a j) -> (k a) j", j=P))
+        nc.sync.dma_start(out=params[0:8, 0:K_PASS], in_=ln_scale.rearrange("k (g c) -> (k g) c", g=PASSES))
+        nc.sync.dma_start(out=params[8:16, 0:K_PASS], in_=ln_bias.rearrange("k (g c) -> (k g) c", g=PASSES))
+        nc.sync.dma_start(out=params[0:64, K_PASS:], in_=b1.rearrange("k (a j) -> (k a) j", j=P))
         scratch = const.tile([P, 1], F32, name="scratch")
         nc.scalar.activation(out=scratch[:], in_=zero[:], func=ACT.Gelu)
 
@@ -82,7 +84,7 @@ def tile_twostepvoicecraftheads_pa_kernel(tc, x, ln_scale, ln_bias, W1, b1, out)
         for k in range(3):
             load_w(k)
 
-        grouped, words, scales, sums, gelus, turned, out_sb = {}, {}, {}, {}, {}, {}, {}
+        bank, grouped, words, scales, sums, gelus, turned, out_sb = {}, {}, {}, {}, {}, {}, {}, {}
 
         def blocks(s):
             if s < ROUNDS_PER_HEAD:
@@ -94,12 +96,29 @@ def tile_twostepvoicecraftheads_pa_kernel(tc, x, ln_scale, ln_bias, W1, b1, out)
             grouped[s] = grouped_pool.tile([P, 2, COLS, PACK], BF16, name="grouped%d" % s, tag="grouped", align_bytes=64)
             for b, (r, g) in enumerate(blocks(s)):
                 k, n = divmod(r, ROUNDS_PER_HEAD)
-                on_scalar = b == 1 and s % SCALAR_EVERY == 1 and s <= SCALAR_LAST
-                copy = nc.scalar.copy if on_scalar else nc.vector.tensor_copy
+                copy = nc.scalar.copy if b == 1 and s in SCALAR_STEPS else nc.vector.tensor_copy
+                width = HALF if b == 1 and s >= TENSOR_FROM else COLS
                 copy(
-                    out=grouped[s][:, b].rearrange("p (c i) t -> p c t i", i=4),
-                    in_=raw[(k, g)][:, :, COLS * n : COLS * (n + 1)].rearrange("p t (c i) -> p c t i", i=4),
+                    out=grouped[s][:, b, 0:width].rearrange("p (c i) t -> p c t i", i=4),
+                    in_=raw[(k, g)][:, :, COLS * n : COLS * n + width].rearrange("p t (c i) -> p c t i", i=4),
                 )
+
+        def regroup_on_tensor(s):
+            r, g = blocks(s)[1]
+            k, n = divmod(r, ROUNDS_PER_HEAD)
+            bank[s] = bank_pool.tile([P, HALF, PACK], BF16, name="bank%d" % s, tag="bank")
+            for j in range(HALF // P):
+                c0 = COLS * n + HALF + j * P
+                nc.tensor.matmul(
+                    out=bank[s][:, j * P : (j + 1) * P, :],
+                    lhsT=ident_bf[:],
+                    rhs=raw[(k, g)][:, :, c0 : c0 + P].rearrange("p t h -> p h t"),
+                    start=True,
+                    stop=True,
+                )
+
+        def copy_bank(s):
+            nc.scalar.copy(out=grouped[s][:, 1, HALF:COLS], in_=bank[s][:])
 
         def quantise(s):
             for b, (r, g) in enumerate(blocks(s)):
@@ -176,48 +195,49 @@ def tile_twostepvoicecraftheads_pa_kernel(tc, x, ln_scale, ln_bias, W1, b1, out)
 
         stats = const.tile([P, TOK_TILES, 2, 6], F32, name="stats")
         mean_var = const.tile([P, TOK_TILES, 2], F32, name="mean_var")
+        var_eps = const.tile([P, TOK_TILES], F32, name="var_eps")
+        rstd = const.tile([P, TOK_TILES], F32, name="rstd")
         for m in range(TOK_TILES):
             for half in range(2):
                 nc.vector.bn_stats(out=stats[:, m, half, :], in_=x_sb[:, m, 512 * half : 512 * (half + 1)])
             nc.vector.bn_aggr(out=mean_var[:, m, :], in_=stats[:, m, :, :].rearrange("p a b -> p (a b)"))
-        var_eps = const.tile([P, TOK_TILES], F32, name="var_eps")
-        nc.vector.tensor_scalar(out=var_eps[:], in0=mean_var[:, :, 1], scalar1=LN_EPS, scalar2=None, op0=ALU.add)
-        minus_mean = const.tile([P, TOK_TILES], F32, name="minus_mean")
-        nc.vector.tensor_scalar(out=minus_mean[:], in0=mean_var[:, :, 0], scalar1=-1.0, scalar2=None, op0=ALU.mult)
-        rstd = const.tile([P, TOK_TILES], F32, name="rstd")
-        nc.gpsimd.tensor_tensor(out=rstd[:], in0=var_eps[:], in1=minus_half[:], op=ALU.pow)
-        shift = const.tile([P, TOK_TILES], F32, name="shift")
-        nc.gpsimd.tensor_tensor(out=shift[:], in0=minus_mean[:], in1=rstd[:], op=ALU.mult)
+            nc.vector.tensor_scalar(
+                out=var_eps[:, m : m + 1], in0=mean_var[:, m, 1:2], scalar1=LN_EPS, scalar2=None, op0=ALU.add
+            )
+            nc.gpsimd.tensor_tensor(
+                out=rstd[:, m : m + 1], in0=var_eps[:, m : m + 1], in1=minus_half[:, m : m + 1], op=ALU.pow
+            )
 
         params_by_t = const.tile([P, PACK, P], BF16, name="params_by_t")
-        nc.vector.tensor_copy(out=params_by_t[:], in_=params[:, 0:K_PASS].rearrange("r (p t) -> r t p", t=PACK))
+        nc.scalar.copy(out=params_by_t[:], in_=params[:, 0:K_PASS].rearrange("r (p t) -> r t p", t=PACK))
         params_ps = sum_pool.tile([P, PACK + 1, P], BF16, name="params_ps", tag="sums")
         for t in range(PACK):
             nc.tensor.transpose(out=params_ps[:, t, :], in_=params_by_t[:, t, :], identity=ident_bf[:])
         nc.tensor.transpose(out=params_ps[:, PACK, :], in_=params[:, K_PASS:], identity=ident_bf[:])
 
-        regroup(0)
-
         ln_col = const.tile([P, PACK, 16], F32, name="ln_col")
-        nc.vector.tensor_copy(out=ln_col[:], in_=params_ps[:, 0:PACK, 0:16])
+        nc.scalar.copy(out=ln_col[:], in_=params_ps[:, 0:PACK, 0:16])
         b1_col = const.tile([P, HEADS * H // P], F32, name="b1_col")
-        nc.vector.tensor_copy(out=b1_col[:], in_=params_ps[:, PACK, 0 : HEADS * H // P])
+        nc.scalar.copy(out=b1_col[:], in_=params_ps[:, PACK, 0 : HEADS * H // P])
 
         xn = const.tile([P, TOK_TILES, PASSES, PACK, P], F32, name="xn")
-        for g in range(PASSES):
-            for m in range(TOK_TILES):
-                nc.scalar.activation(
+        for m in range(TOK_TILES):
+            for g in range(PASSES):
+                nc.vector.tensor_scalar(
                     out=xn[:, m, g],
-                    in_=x_sb[:, m, K_PASS * g : K_PASS * (g + 1)].rearrange("n (p t) -> n t p", t=PACK),
-                    func=ACT.Identity,
-                    scale=rstd[:, m : m + 1],
-                    bias=shift[:, m : m + 1],
+                    in0=x_sb[:, m, K_PASS * g : K_PASS * (g + 1)].rearrange("n (p t) -> n t p", t=PACK),
+                    scalar1=mean_var[:, m, 0:1],
+                    scalar2=rstd[:, m : m + 1],
+                    op0=ALU.subtract,
+                    op1=ALU.mult,
                 )
+        regroup(0)
         xn_t = {}
         for g in range(PASSES):
             for t in range(PACK):
                 if t % 2 == 0:
-                    xn_t[(g, t // 2)] = turn_pool.tile([P, 2, TOK], F32, name="xn_t%d_%d" % (g, t // 2), tag="turned")
+                    pool, tag = (sum_pool, "sums") if (g, t) == (1, 2) else (turn_pool, "turned")
+                    xn_t[(g, t // 2)] = pool.tile([P, 2, TOK], F32, name="xn_t%d_%d" % (g, t // 2), tag=tag)
                 for m in range(TOK_TILES):
                     nc.tensor.transpose(
                         out=xn_t[(g, t // 2)][:, t % 2, m * P : (m + 1) * P],
@@ -262,26 +282,38 @@ def tile_twostepvoicecraftheads_pa_kernel(tc, x, ln_scale, ln_bias, W1, b1, out)
         for k in range(HEADS):
             affine(k)
             regroup(k + 2)
+            if k + 2 >= TENSOR_FROM:
+                regroup_on_tensor(k + 2)
+                copy_bank(k + 2)
             if k == 1:
                 load_w(3)
             if k >= 1:
                 y_quantise(k - 1)
             quantise(k + 1)
             y_regroup(k)
+            if k == 1:
+                multiply(0)
         regroup(HEADS + 2)
+        if HEADS + 2 >= TENSOR_FROM:
+            regroup_on_tensor(HEADS + 2)
+            copy_bank(HEADS + 2)
         y_quantise(HEADS - 1)
-        multiply(0)
 
         for i in range(ROUNDS + 1):
             if i >= 1:
                 turn_back(i - 1)
-            if i + 1 < ROUNDS:
-                multiply(i + 1)
+            on_tensor = max(PROLOGUE_REGROUPED, TENSOR_FROM) <= i + LEAD < ROUNDS
             if PROLOGUE_REGROUPED <= i + LEAD < ROUNDS:
                 regroup(i + LEAD)
+            if i + 1 < ROUNDS:
+                multiply(i + 1)
+            if on_tensor:
+                regroup_on_tensor(i + LEAD)
             if PROLOGUE_QUANTISED <= i + LEAD - 1 < ROUNDS:
                 quantise(i + LEAD - 1)
             if i < ROUNDS:
                 bias_gelu(i)
             if i >= 1:
                 copy_out_and_store(i - 1)
+            if on_tensor:
+                copy_bank(i + LEAD)

@@ -30,8 +30,7 @@ FLOPS = 2 * TOK * D * H * HEADS
 SCALAR_STEPS = (1, 3)
 TENSOR_FROM = 4
 HALF = COLS // 2
-VECTOR_ONE_COPY_FROM = ROUNDS - 4
-VECTOR_BOTH_COPIES_FROM = ROUNDS - 2
+TOKENS_FROM = ROUNDS - 4
 PROLOGUE_REGROUPED = HEADS + 3
 PROLOGUE_QUANTISED = HEADS + 1
 LEAD = 5
@@ -110,9 +109,9 @@ def tile_twostepvoicecraftheads_pa_kernel(tc, x, ln_scale, ln_bias, W1, b1, out)
             for j in range(HALF // P):
                 c0 = COLS * n + HALF + j * P
                 nc.tensor.matmul(
-                    out=bank[s][:, j * P : (j + 1) * P, :],
+                    out=bank[s][:, j * P : (j + 1) * P, :].rearrange("p h t -> p t h"),
                     lhsT=ident_bf[:],
-                    rhs=raw[(k, g)][:, :, c0 : c0 + P].rearrange("p t h -> p h t"),
+                    rhs=raw[(k, g)][:, :, c0 : c0 + P],
                     start=True,
                     stop=True,
                 )
@@ -133,6 +132,21 @@ def tile_twostepvoicecraftheads_pa_kernel(tc, x, ln_scale, ln_bias, W1, b1, out)
 
         def multiply(r):
             k = r // ROUNDS_PER_HEAD
+            if r >= TOKENS_FROM:
+                sums[r] = [sum_pool.tile([P, COLS], F32, name="sums%d_%d" % (r, m), tag="sums") for m in range(TOK_TILES)]
+                for m in range(TOK_TILES):
+                    for g in range(PASSES):
+                        tokens = slice(g * TOK + m * P, g * TOK + (m + 1) * P)
+                        nc.tensor.matmul_mx(
+                            out=sums[r][m][:],
+                            lhsT=y_words[:, k, tokens].bitcast(FP8X4),
+                            lhsT_scale=y_scales[:, k, tokens],
+                            rhs=words[r][:, g * COLS : (g + 1) * COLS].bitcast(FP8X4),
+                            rhs_scale=scales[r][:, g * COLS : (g + 1) * COLS],
+                            start=(g == 0),
+                            stop=(g == PASSES - 1),
+                        )
+                return
             sums[r] = [sum_pool.tile([P, 2, TOK], F32, name="sums%d_%d" % (r, a), tag="sums") for a in range(H_TILES // 2)]
             for a in range(H_TILES):
                 for g in range(PASSES):
@@ -159,6 +173,25 @@ def tile_twostepvoicecraftheads_pa_kernel(tc, x, ln_scale, ln_bias, W1, b1, out)
                     scale=1.0,
                 )
 
+        def add_gelu_and_store(r):
+            k, n = divmod(r, ROUNDS_PER_HEAD)
+            pair, second = divmod(n, 2)
+            if not second:
+                out_sb[(k, pair)] = [
+                    out_pool.tile([P, 2 * COLS], F32, name="out%d_%d_%d" % (k, pair, m), tag="out") for m in range(TOK_TILES)
+                ]
+            c0, c1 = second * COLS, (second + 1) * COLS
+            for m in range(TOK_TILES):
+                piece = out_sb[(k, pair)][m][:, c0:c1]
+                nc.vector.tensor_tensor(out=piece, in0=sums[r][m][:], in1=b1_row[:, (r - TOKENS_FROM) * COLS : (r - TOKENS_FROM + 1) * COLS], op=ALU.add)
+            for m in range(TOK_TILES):
+                piece = out_sb[(k, pair)][m][:, c0:c1]
+                nc.scalar.activation(out=piece, in_=piece, func=ACT.Gelu)
+                for e in range(2):
+                    nc.sync.dma_start(
+                        out=out[2 * m + e, k, :, n * COLS : (n + 1) * COLS], in_=out_sb[(k, pair)][m][e:P:2, c0:c1]
+                    )
+
         def turn_back(r):
             turned[r] = [turn_pool.tile([P, COLS], F32, name="turned%d_%d" % (r, m), tag="turned") for m in range(TOK_TILES)]
             for a in range(H_TILES):
@@ -177,12 +210,8 @@ def tile_twostepvoicecraftheads_pa_kernel(tc, x, ln_scale, ln_bias, W1, b1, out)
                     out_pool.tile([P, 2 * COLS], F32, name="out%d_%d_%d" % (k, pair, m), tag="out") for m in range(TOK_TILES)
                 ]
             for m in range(TOK_TILES):
-                on_vector = r >= VECTOR_BOTH_COPIES_FROM or (r >= VECTOR_ONE_COPY_FROM and m == 0)
-                copy = nc.vector.tensor_copy if on_vector else nc.scalar.copy
-                copy(out=out_sb[(k, pair)][m][:, second * COLS : (second + 1) * COLS], in_=turned[r][m][:])
-            if r >= ROUNDS - 2:
-                c0, c1 = second * COLS, (second + 1) * COLS
-            elif second:
+                nc.scalar.copy(out=out_sb[(k, pair)][m][:, second * COLS : (second + 1) * COLS], in_=turned[r][m][:])
+            if second:
                 c0, c1 = 0, 2 * COLS
             else:
                 return
@@ -207,6 +236,11 @@ def tile_twostepvoicecraftheads_pa_kernel(tc, x, ln_scale, ln_bias, W1, b1, out)
             nc.gpsimd.tensor_tensor(
                 out=rstd[:, m : m + 1], in0=var_eps[:, m : m + 1], in1=minus_half[:, m : m + 1], op=ALU.pow
             )
+        shift = const.tile([P, TOK_TILES], F32, name="shift")
+        for m in range(TOK_TILES):
+            nc.vector.scalar_tensor_tensor(
+                out=shift[:, m : m + 1], in0=mean_var[:, m, 0:1], scalar=-1.0, in1=rstd[:, m : m + 1], op0=ALU.mult, op1=ALU.mult
+            )
 
         params_by_t = const.tile([P, PACK, P], BF16, name="params_by_t")
         nc.scalar.copy(out=params_by_t[:], in_=params[:, 0:K_PASS].rearrange("r (p t) -> r t p", t=PACK))
@@ -223,13 +257,12 @@ def tile_twostepvoicecraftheads_pa_kernel(tc, x, ln_scale, ln_bias, W1, b1, out)
         xn = const.tile([P, TOK_TILES, PASSES, PACK, P], F32, name="xn")
         for m in range(TOK_TILES):
             for g in range(PASSES):
-                nc.vector.tensor_scalar(
+                nc.scalar.activation(
                     out=xn[:, m, g],
-                    in0=x_sb[:, m, K_PASS * g : K_PASS * (g + 1)].rearrange("n (p t) -> n t p", t=PACK),
-                    scalar1=mean_var[:, m, 0:1],
-                    scalar2=rstd[:, m : m + 1],
-                    op0=ALU.subtract,
-                    op1=ALU.mult,
+                    in_=x_sb[:, m, K_PASS * g : K_PASS * (g + 1)].rearrange("n (p t) -> n t p", t=PACK),
+                    func=ACT.Identity,
+                    scale=rstd[:, m : m + 1],
+                    bias=shift[:, m : m + 1],
                 )
         regroup(0)
         xn_t = {}
@@ -287,6 +320,8 @@ def tile_twostepvoicecraftheads_pa_kernel(tc, x, ln_scale, ln_bias, W1, b1, out)
                 copy_bank(k + 2)
             if k == 1:
                 load_w(3)
+                b1_row = const.tile([P, (ROUNDS - TOKENS_FROM) * COLS], BF16, name="b1_row")
+                nc.sync.dma_start(out=b1_row[:], in_=b1[HEADS - 1, H - (ROUNDS - TOKENS_FROM) * COLS :].partition_broadcast(P))
             if k >= 1:
                 y_quantise(k - 1)
             quantise(k + 1)
@@ -299,8 +334,8 @@ def tile_twostepvoicecraftheads_pa_kernel(tc, x, ln_scale, ln_bias, W1, b1, out)
             copy_bank(HEADS + 2)
         y_quantise(HEADS - 1)
 
-        for i in range(ROUNDS + 1):
-            if i >= 1:
+        for i in range(ROUNDS):
+            if 1 <= i <= TOKENS_FROM:
                 turn_back(i - 1)
             on_tensor = max(PROLOGUE_REGROUPED, TENSOR_FROM) <= i + LEAD < ROUNDS
             if PROLOGUE_REGROUPED <= i + LEAD < ROUNDS:
@@ -311,9 +346,11 @@ def tile_twostepvoicecraftheads_pa_kernel(tc, x, ln_scale, ln_bias, W1, b1, out)
                 regroup_on_tensor(i + LEAD)
             if PROLOGUE_QUANTISED <= i + LEAD - 1 < ROUNDS:
                 quantise(i + LEAD - 1)
-            if i < ROUNDS:
+            if i < TOKENS_FROM:
                 bias_gelu(i)
-            if i >= 1:
+            if 1 <= i <= TOKENS_FROM:
                 copy_out_and_store(i - 1)
+            if i >= TOKENS_FROM:
+                add_gelu_and_store(i)
             if on_tensor:
                 copy_bank(i + LEAD)

@@ -57,8 +57,6 @@ def tile_twostepvoicecraftheads_pa_kernel(tc, x, ln_scale, ln_bias, W1, b1, out)
         nc.vector.memset(params[:].bitcast(I32), 0)
         ident_bf = const.tile([P, P], BF16, name="ident_bf")
         nc.vector.tensor_copy(out=ident_bf[:], in_=ident[:])
-        minus_half = const.tile([P, TOK_TILES], F32, name="minus_half")
-        nc.vector.memset(minus_half[:], -0.5)
         zero = const.tile([P, 1], F32, name="zero")
         nc.vector.memset(zero[:], 0.0)
 
@@ -70,15 +68,24 @@ def tile_twostepvoicecraftheads_pa_kernel(tc, x, ln_scale, ln_bias, W1, b1, out)
         nc.sync.dma_start(out=params[8:16, 0:K_PASS], in_=ln_bias.rearrange("k (g c) -> (k g) c", g=PASSES))
         nc.sync.dma_start(out=params[0:64, K_PASS:], in_=b1.rearrange("k (a j) -> (k a) j", j=P))
         scratch = const.tile([P, 1], F32, name="scratch")
-        nc.scalar.activation(out=scratch[:], in_=zero[:], func=ACT.Gelu)
+        nc.scalar.activation(out=scratch[:], in_=zero[:], func=ACT.Sqrt)
 
         raw = {}
 
         def load_w(k):
+            parts = 2 if k == 0 else 1
+            width = H // parts
             for g in range(PASSES):
-                raw[(k, g)] = raw_pool.tile([P, PACK, H], BF16, name="raw%d_%d" % (k, g), tag="raw")
-                rows = W1[k, K_PASS * g : K_PASS * (g + 1), :].rearrange("(p t) h -> p t h", t=PACK)
-                nc.sync.dma_start(out=raw[(k, g)][:], in_=rows)
+                raw[(k, g)] = raw_pool.tile([P, parts, PACK, width], BF16, name="raw%d_%d" % (k, g), tag="raw")
+            for part in range(parts):
+                for g in range(PASSES):
+                    rows = W1[k, K_PASS * g : K_PASS * (g + 1), :].rearrange("(p t) h -> p t h", t=PACK)
+                    nc.sync.dma_start(out=raw[(k, g)][:, part], in_=rows[:, :, part * width : (part + 1) * width])
+
+        def columns(k, g, c0, width):
+            part_width = raw[(k, g)].shape[3]
+            part, first = divmod(c0, part_width)
+            return raw[(k, g)][:, part, :, first : first + width]
 
         for k in range(3):
             load_w(k)
@@ -87,20 +94,25 @@ def tile_twostepvoicecraftheads_pa_kernel(tc, x, ln_scale, ln_bias, W1, b1, out)
 
         def blocks(s):
             if s < ROUNDS_PER_HEAD:
-                g, r = divmod(2 * s, ROUNDS_PER_HEAD)
-                return [(r, g), (r + 1, g)]
+                half, g = divmod(s, PASSES)
+                return [(2 * half, g), (2 * half + 1, g)]
             return [(s, 0), (s, 1)]
 
         def regroup(s):
-            grouped[s] = grouped_pool.tile([P, 2, COLS, PACK], BF16, name="grouped%d" % s, tag="grouped", align_bytes=64)
-            for b, (r, g) in enumerate(blocks(s)):
-                k, n = divmod(r, ROUNDS_PER_HEAD)
-                copy = nc.scalar.copy if b == 1 and s in SCALAR_STEPS else nc.vector.tensor_copy
-                width = HALF if b == 1 and s >= TENSOR_FROM else COLS
-                copy(
-                    out=grouped[s][:, b, 0:width].rearrange("p (c i) t -> p c t i", i=4),
-                    in_=raw[(k, g)][:, :, COLS * n : COLS * n + width].rearrange("p t (c i) -> p c t i", i=4),
-                )
+            for b in range(2):
+                regroup_block(s, b)
+
+        def regroup_block(s, b):
+            if b == 0:
+                grouped[s] = grouped_pool.tile([P, 2, COLS, PACK], BF16, name="grouped%d" % s, tag="grouped", align_bytes=64)
+            r, g = blocks(s)[b]
+            k, n = divmod(r, ROUNDS_PER_HEAD)
+            copy = nc.scalar.copy if b == 1 and s in SCALAR_STEPS else nc.vector.tensor_copy
+            width = HALF if b == 1 and s >= TENSOR_FROM else COLS
+            copy(
+                out=grouped[s][:, b, 0:width].rearrange("p (c i) t -> p c t i", i=4),
+                in_=columns(k, g, COLS * n, width).rearrange("p t (c i) -> p c t i", i=4),
+            )
 
         def regroup_on_tensor(s):
             r, g = blocks(s)[1]
@@ -111,7 +123,7 @@ def tile_twostepvoicecraftheads_pa_kernel(tc, x, ln_scale, ln_bias, W1, b1, out)
                 nc.tensor.matmul(
                     out=bank[s][:, j * P : (j + 1) * P, :].rearrange("p h t -> p t h"),
                     lhsT=ident_bf[:],
-                    rhs=raw[(k, g)][:, :, c0 : c0 + P],
+                    rhs=columns(k, g, c0, P),
                     start=True,
                     stop=True,
                 )
@@ -222,26 +234,6 @@ def tile_twostepvoicecraftheads_pa_kernel(tc, x, ln_scale, ln_bias, W1, b1, out)
                         in_=out_sb[(k, pair)][m][e:P:2, c0:c1],
                     )
 
-        stats = const.tile([P, TOK_TILES, 2, 6], F32, name="stats")
-        mean_var = const.tile([P, TOK_TILES, 2], F32, name="mean_var")
-        var_eps = const.tile([P, TOK_TILES], F32, name="var_eps")
-        rstd = const.tile([P, TOK_TILES], F32, name="rstd")
-        for m in range(TOK_TILES):
-            for half in range(2):
-                nc.vector.bn_stats(out=stats[:, m, half, :], in_=x_sb[:, m, 512 * half : 512 * (half + 1)])
-            nc.vector.bn_aggr(out=mean_var[:, m, :], in_=stats[:, m, :, :].rearrange("p a b -> p (a b)"))
-            nc.vector.tensor_scalar(
-                out=var_eps[:, m : m + 1], in0=mean_var[:, m, 1:2], scalar1=LN_EPS, scalar2=None, op0=ALU.add
-            )
-            nc.gpsimd.tensor_tensor(
-                out=rstd[:, m : m + 1], in0=var_eps[:, m : m + 1], in1=minus_half[:, m : m + 1], op=ALU.pow
-            )
-        shift = const.tile([P, TOK_TILES], F32, name="shift")
-        for m in range(TOK_TILES):
-            nc.vector.scalar_tensor_tensor(
-                out=shift[:, m : m + 1], in0=mean_var[:, m, 0:1], scalar=-1.0, in1=rstd[:, m : m + 1], op0=ALU.mult, op1=ALU.mult
-            )
-
         params_by_t = const.tile([P, PACK, P], BF16, name="params_by_t")
         nc.scalar.copy(out=params_by_t[:], in_=params[:, 0:K_PASS].rearrange("r (p t) -> r t p", t=PACK))
         params_ps = sum_pool.tile([P, PACK + 1, P], BF16, name="params_ps", tag="sums")
@@ -249,10 +241,36 @@ def tile_twostepvoicecraftheads_pa_kernel(tc, x, ln_scale, ln_bias, W1, b1, out)
             nc.tensor.transpose(out=params_ps[:, t, :], in_=params_by_t[:, t, :], identity=ident_bf[:])
         nc.tensor.transpose(out=params_ps[:, PACK, :], in_=params[:, K_PASS:], identity=ident_bf[:])
 
-        ln_col = const.tile([P, PACK, 16], F32, name="ln_col")
-        nc.scalar.copy(out=ln_col[:], in_=params_ps[:, 0:PACK, 0:16])
-        b1_col = const.tile([P, HEADS * H // P], F32, name="b1_col")
-        nc.scalar.copy(out=b1_col[:], in_=params_ps[:, PACK, 0 : HEADS * H // P])
+        stats = const.tile([P, TOK_TILES, 2, 6], F32, name="stats")
+        mean_var = const.tile([P, TOK_TILES, 2], F32, name="mean_var")
+        std = const.tile([P, TOK_TILES], F32, name="std")
+        rstd = const.tile([P, TOK_TILES], F32, name="rstd")
+        shift = const.tile([P, TOK_TILES], F32, name="shift")
+
+        def moments(m, half):
+            nc.vector.bn_stats(out=stats[:, m, half, :], in_=x_sb[:, m, 512 * half : 512 * (half + 1)])
+
+        def aggregate(m):
+            nc.vector.bn_aggr(out=mean_var[:, m, :], in_=stats[:, m, :, :].rearrange("p a b -> p (a b)"))
+            nc.scalar.activation(out=std[:, m : m + 1], in_=mean_var[:, m, 1:2], func=ACT.Sqrt, bias=LN_EPS, scale=1.0)
+
+        def invert(m):
+            nc.vector.reciprocal(out=rstd[:, m : m + 1], in_=std[:, m : m + 1])
+            nc.vector.scalar_tensor_tensor(
+                out=shift[:, m : m + 1], in0=mean_var[:, m, 0:1], scalar=-1.0, in1=rstd[:, m : m + 1], op0=ALU.mult, op1=ALU.mult
+            )
+
+        moments(0, 0)
+        moments(0, 1)
+        moments(1, 0)
+        aggregate(0)
+        moments(1, 1)
+        invert(0)
+        aggregate(1)
+        nc.scalar.activation(out=scratch[:], in_=zero[:], func=ACT.Gelu)
+        regroup_block(0, 0)
+        invert(1)
+        regroup_block(0, 1)
 
         xn = const.tile([P, TOK_TILES, PASSES, PACK, P], F32, name="xn")
         for m in range(TOK_TILES):
@@ -264,7 +282,11 @@ def tile_twostepvoicecraftheads_pa_kernel(tc, x, ln_scale, ln_bias, W1, b1, out)
                     scale=rstd[:, m : m + 1],
                     bias=shift[:, m : m + 1],
                 )
-        regroup(0)
+        ln_col = const.tile([P, PACK, 16], F32, name="ln_col")
+        nc.scalar.copy(out=ln_col[:], in_=params_ps[:, 0:PACK, 0:16])
+        b1_col = const.tile([P, HEADS * H // P], F32, name="b1_col")
+        nc.scalar.copy(out=b1_col[:], in_=params_ps[:, PACK, 0 : HEADS * H // P])
+
         xn_t = {}
         for g in range(PASSES):
             for t in range(PACK):

@@ -96,6 +96,9 @@ def tile_twostepvoicecraftheads_pa_kernel(tc, x, ln_scale, ln_bias, W1, b1, out)
             if s < ROUNDS_PER_HEAD:
                 half, g = divmod(s, PASSES)
                 return [(2 * half, g), (2 * half + 1, g)]
+            if s < ROUNDS_PER_HEAD + 2:
+                g = s - ROUNDS_PER_HEAD
+                return [(ROUNDS_PER_HEAD, g), (ROUNDS_PER_HEAD + 1, g)]
             return [(s, 0), (s, 1)]
 
         def regroup(s):
@@ -353,7 +356,6 @@ def tile_twostepvoicecraftheads_pa_kernel(tc, x, ln_scale, ln_bias, W1, b1, out)
         regroup(HEADS + 2)
         if HEADS + 2 >= TENSOR_FROM:
             regroup_on_tensor(HEADS + 2)
-            copy_bank(HEADS + 2)
         y_quantise(HEADS - 1)
 
         for i in range(ROUNDS):
@@ -370,6 +372,8 @@ def tile_twostepvoicecraftheads_pa_kernel(tc, x, ln_scale, ln_bias, W1, b1, out)
                 quantise(i + LEAD - 1)
             if i < TOKENS_FROM:
                 bias_gelu(i)
+            if i == 0:
+                copy_bank(HEADS + 2)
             if 1 <= i <= TOKENS_FROM:
                 copy_out_and_store(i - 1)
             if i >= TOKENS_FROM:

from contextlib import ExitStack

import concourse.mybir as mybir
from concourse.masks import make_identity

F32 = mybir.dt.float32
BF16 = mybir.dt.bfloat16
U32 = mybir.dt.uint32
U8 = mybir.dt.uint8
I32 = mybir.dt.int32
FP8X4 = mybir.dt.float8_e4m3fn_x4
ACT = mybir.ActivationFunctionType
ALU = mybir.AluOpType

P = 128
PACK = 4
K_PASS = P * PACK
HEADS, D, H, BATCH, T = 4, 1024, 2048, 4, 64
LN_EPS = 1e-5
PASSES = D // K_PASS
TOK = BATCH * T
TOK_TILES = TOK // P
COLS = 512
H_TILES = COLS // P
ROUNDS_PER_HEAD = H // COLS
ROUNDS = HEADS * ROUNDS_PER_HEAD

FLOPS = 2 * TOK * D * H * HEADS

SCALAR_STEPS = (1, 3)
TENSOR_FROM = 4
HALF = COLS // 2
TOKENS_FROM = ROUNDS - 4
PROLOGUE_REGROUPED = HEADS + 3
PROLOGUE_QUANTISED = HEADS + 1
LEAD = 5


def tile_twostepvoicecraftheads_pa_kernel(tc, x, ln_scale, ln_bias, W1, b1, out):
    nc = tc.nc
    with ExitStack() as ctx:
        const = ctx.enter_context(tc.tile_pool(name="const", bufs=1))
        raw_pool = ctx.enter_context(tc.tile_pool(name="raw", bufs=6))
        grouped_pool = ctx.enter_context(tc.tile_pool(name="grouped", bufs=3))
        words_pool = ctx.enter_context(tc.tile_pool(name="words", bufs=PROLOGUE_QUANTISED))
        y_pool = ctx.enter_context(tc.tile_pool(name="y", bufs=2))
        gelu_pool = ctx.enter_context(tc.tile_pool(name="gelu", bufs=3))
        out_pool = ctx.enter_context(tc.tile_pool(name="outp", bufs=8))
        sum_pool = ctx.enter_context(tc.psum_pool(name="sums", bufs=4))
        bank_pool = ctx.enter_context(tc.psum_pool(name="bank", bufs=1))
        turn_pool = ctx.enter_context(tc.psum_pool(name="turned", bufs=3))
        ctx.enter_context(tc.manual_schedule())

        ident = const.tile([P, P], F32, name="ident")
        make_identity(nc, ident[:])
        params = const.tile([P, K_PASS + P], BF16, name="params")
        nc.vector.memset(params[:].bitcast(I32), 0)
        ident_bf = const.tile([P, P], BF16, name="ident_bf")
        nc.vector.tensor_copy(out=ident_bf[:], in_=ident[:])
        zero = const.tile([P, 1], F32, name="zero")
        nc.vector.memset(zero[:], 0.0)

        x_sb = const.tile([P, TOK_TILES, D], BF16, name="x_sb")
        for m in range(TOK_TILES):
            for e in range(2):
                nc.sync.dma_start(out=x_sb[e:P:2, m, :], in_=x[2 * m + e])
        nc.sync.dma_start(out=params[0:8, 0:K_PASS], in_=ln_scale.rearrange("k (g c) -> (k g) c", g=PASSES))
        nc.sync.dma_start(out=params[8:16, 0:K_PASS], in_=ln_bias.rearrange("k (g c) -> (k g) c", g=PASSES))
        nc.sync.dma_start(out=params[0:64, K_PASS:], in_=b1.rearrange("k (a j) -> (k a) j", j=P))
        scratch = const.tile([P, 1], F32, name="scratch")
        nc.scalar.activation(out=scratch[:], in_=zero[:], func=ACT.Sqrt)

        raw = {}

        def load_w(k):
            parts = 2 if k == 0 else 1
            width = H // parts
            for g in range(PASSES):
                raw[(k, g)] = raw_pool.tile([P, parts, PACK, width], BF16, name="raw%d_%d" % (k, g), tag="raw")
            for part in range(parts):
                for g in range(PASSES):
                    rows = W1[k, K_PASS * g : K_PASS * (g + 1), :].rearrange("(p t) h -> p t h", t=PACK)
                    nc.sync.dma_start(out=raw[(k, g)][:, part], in_=rows[:, :, part * width : (part + 1) * width])

        def columns(k, g, c0, width):
            part_width = raw[(k, g)].shape[3]
            part, first = divmod(c0, part_width)
            return raw[(k, g)][:, part, :, first : first + width]

        for k in range(3):
            load_w(k)

        bank, grouped, words, scales, sums, gelus, turned, out_sb = {}, {}, {}, {}, {}, {}, {}, {}

        def blocks(s):
            if s < ROUNDS_PER_HEAD:
                half, g = divmod(s, PASSES)
                return [(2 * half, g), (2 * half + 1, g)]
            if s < ROUNDS_PER_HEAD + 2:
                g = s - ROUNDS_PER_HEAD
                return [(ROUNDS_PER_HEAD, g), (ROUNDS_PER_HEAD + 1, g)]
            return [(s, 0), (s, 1)]

        def regroup(s):
            for b in range(2):
                regroup_block(s, b)

        def regroup_block(s, b):
            if b == 0:
                grouped[s] = grouped_pool.tile([P, 2, COLS, PACK], BF16, name="grouped%d" % s, tag="grouped", align_bytes=64)
            r, g = blocks(s)[b]
            k, n = divmod(r, ROUNDS_PER_HEAD)
            copy = nc.scalar.copy if b == 1 and s in SCALAR_STEPS else nc.vector.tensor_copy
            width = HALF if b == 1 and s >= TENSOR_FROM else COLS
            copy(
                out=grouped[s][:, b, 0:width].rearrange("p (c i) t -> p c t i", i=4),
                in_=columns(k, g, COLS * n, width).rearrange("p t (c i) -> p c t i", i=4),
            )

        def regroup_on_tensor(s):
            r, g = blocks(s)[1]
            k, n = divmod(r, ROUNDS_PER_HEAD)
            bank[s] = bank_pool.tile([P, HALF, PACK], BF16, name="bank%d" % s, tag="bank")
            for j in range(HALF // P):
                c0 = COLS * n + HALF + j * P
                nc.tensor.matmul(
                    out=bank[s][:, j * P : (j + 1) * P, :].rearrange("p h t -> p t h"),
                    lhsT=ident_bf[:],
                    rhs=columns(k, g, c0, P),
                    start=True,
                    stop=True,
                )

        def copy_bank(s):
            nc.scalar.copy(out=grouped[s][:, 1, HALF:COLS], in_=bank[s][:])

        def quantise(s):
            for b, (r, g) in enumerate(blocks(s)):
                if r not in words:
                    words[r] = words_pool.tile([P, PASSES * COLS], U32, name="words%d" % r, tag="words", align_bytes=64)
                    scales[r] = words_pool.tile([P, PASSES * COLS], U8, name="scales%d" % r, tag="scales", align_bytes=64)
                nc.vector.quantize_mx(
                    out=words[r][:, g * COLS : (g + 1) * COLS].bitcast(FP8X4),
                    scales=scales[r][:, g * COLS : (g + 1) * COLS],
                    in_=grouped[s][:, b].rearrange("p h t -> p (h t)"),
                )

        def multiply(r):
            k = r // ROUNDS_PER_HEAD
            if r >= TOKENS_FROM:
                sums[r] = [sum_pool.tile([P, COLS], F32, name="sums%d_%d" % (r, m), tag="sums") for m in range(TOK_TILES)]
                for m in range(TOK_TILES):
                    for g in range(PASSES):
                        tokens = slice(g * TOK + m * P, g * TOK + (m + 1) * P)
                        nc.tensor.matmul_mx(
                            out=sums[r][m][:],
                            lhsT=y_words[:, k, tokens].bitcast(FP8X4),
                            lhsT_scale=y_scales[:, k, tokens],
                            rhs=words[r][:, g * COLS : (g + 1) * COLS].bitcast(FP8X4),
                            rhs_scale=scales[r][:, g * COLS : (g + 1) * COLS],
                            start=(g == 0),
                            stop=(g == PASSES - 1),
                        )
                return
            sums[r] = [sum_pool.tile([P, 2, TOK], F32, name="sums%d_%d" % (r, a), tag="sums") for a in range(H_TILES // 2)]
            for a in range(H_TILES):
                for g in range(PASSES):
                    h_cols = slice(g * COLS + a * P, g * COLS + (a + 1) * P)
                    tokens = slice(g * TOK, (g + 1) * TOK)
                    nc.tensor.matmul_mx(
                        out=sums[r][a // 2][:, a % 2, :],
                        lhsT=words[r][:, h_cols].bitcast(FP8X4),
                        lhsT_scale=scales[r][:, h_cols],
                        rhs=y_words[:, k, tokens].bitcast(FP8X4),
                        rhs_scale=y_scales[:, k, tokens],
                        start=(g == 0),
                        stop=(g == PASSES - 1),
                    )

        def bias_gelu(r):
            gelus[r] = gelu_pool.tile([P, H_TILES, TOK], F32, name="gelus%d" % r, tag="gelus")
            for a in range(H_TILES):
                nc.scalar.activation(
                    out=gelus[r][:, a, :],
                    in_=sums[r][a // 2][:, a % 2, :],
                    func=ACT.Gelu,
                    bias=b1_col[:, H_TILES * r + a : H_TILES * r + a + 1],
                    scale=1.0,
                )

        def add_gelu_and_store(r):
            k, n = divmod(r, ROUNDS_PER_HEAD)
            pair, second = divmod(n, 2)
            if not second:
                out_sb[(k, pair)] = [
                    out_pool.tile([P, 2 * COLS], F32, name="out%d_%d_%d" % (k, pair, m), tag="out") for m in range(TOK_TILES)
                ]
            c0, c1 = second * COLS, (second + 1) * COLS
            for m in range(TOK_TILES):
                piece = out_sb[(k, pair)][m][:, c0:c1]
                nc.vector.tensor_tensor(out=piece, in0=sums[r][m][:], in1=b1_row[:, (r - TOKENS_FROM) * COLS : (r - TOKENS_FROM + 1) * COLS], op=ALU.add)
            for m in range(TOK_TILES):
                piece = out_sb[(k, pair)][m][:, c0:c1]
                nc.scalar.activation(out=piece, in_=piece, func=ACT.Gelu)
                for e in range(2):
                    nc.sync.dma_start(
                        out=out[2 * m + e, k, :, n * COLS : (n + 1) * COLS], in_=out_sb[(k, pair)][m][e:P:2, c0:c1]
                    )

        def turn_back(r):
            turned[r] = [turn_pool.tile([P, COLS], F32, name="turned%d_%d" % (r, m), tag="turned") for m in range(TOK_TILES)]
            for a in range(H_TILES):
                for m in range(TOK_TILES):
                    nc.tensor.transpose(
                        out=turned[r][m][:, a * P : (a + 1) * P],
                        in_=gelus[r][:, a, m * P : (m + 1) * P],
                        identity=ident[:],
                    )

        def copy_out_and_store(r):
            k, n = divmod(r, ROUNDS_PER_HEAD)
            pair, second = divmod(n, 2)
            if not second:
                out_sb[(k, pair)] = [
                    out_pool.tile([P, 2 * COLS], F32, name="out%d_%d_%d" % (k, pair, m), tag="out") for m in range(TOK_TILES)
                ]
            for m in range(TOK_TILES):
                nc.scalar.copy(out=out_sb[(k, pair)][m][:, second * COLS : (second + 1) * COLS], in_=turned[r][m][:])
            if second:
                c0, c1 = 0, 2 * COLS
            else:
                return
            for m in range(TOK_TILES):
                for e in range(2):
                    nc.sync.dma_start(
                        out=out[2 * m + e, k, :, 2 * COLS * pair + c0 : 2 * COLS * pair + c1],
                        in_=out_sb[(k, pair)][m][e:P:2, c0:c1],
                    )

        params_by_t = const.tile([P, PACK, P], BF16, name="params_by_t")
        nc.scalar.copy(out=params_by_t[:], in_=params[:, 0:K_PASS].rearrange("r (p t) -> r t p", t=PACK))
        params_ps = sum_pool.tile([P, PACK + 1, P], BF16, name="params_ps", tag="sums")
        for t in range(PACK):
            nc.tensor.transpose(out=params_ps[:, t, :], in_=params_by_t[:, t, :], identity=ident_bf[:])
        nc.tensor.transpose(out=params_ps[:, PACK, :], in_=params[:, K_PASS:], identity=ident_bf[:])

        stats = const.tile([P, TOK_TILES, 2, 6], F32, name="stats")
        mean_var = const.tile([P, TOK_TILES, 2], F32, name="mean_var")
        std = const.tile([P, TOK_TILES], F32, name="std")
        rstd = const.tile([P, TOK_TILES], F32, name="rstd")
        shift = const.tile([P, TOK_TILES], F32, name="shift")

        def moments(m, half):
            nc.vector.bn_stats(out=stats[:, m, half, :], in_=x_sb[:, m, 512 * half : 512 * (half + 1)])

        def aggregate(m):
            nc.vector.bn_aggr(out=mean_var[:, m, :], in_=stats[:, m, :, :].rearrange("p a b -> p (a b)"))
            nc.scalar.activation(out=std[:, m : m + 1], in_=mean_var[:, m, 1:2], func=ACT.Sqrt, bias=LN_EPS, scale=1.0)

        def invert(m):
            nc.vector.reciprocal(out=rstd[:, m : m + 1], in_=std[:, m : m + 1])
            nc.vector.scalar_tensor_tensor(
                out=shift[:, m : m + 1], in0=mean_var[:, m, 0:1], scalar=-1.0, in1=rstd[:, m : m + 1], op0=ALU.mult, op1=ALU.mult
            )

        moments(0, 0)
        moments(0, 1)
        moments(1, 0)
        aggregate(0)
        moments(1, 1)
        invert(0)
        aggregate(1)
        nc.scalar.activation(out=scratch[:], in_=zero[:], func=ACT.Gelu)
        regroup_block(0, 0)
        invert(1)
        regroup_block(0, 1)

        xn = const.tile([P, TOK_TILES, PASSES, PACK, P], F32, name="xn")
        for m in range(TOK_TILES):
            for g in range(PASSES):
                nc.scalar.activation(
                    out=xn[:, m, g],
                    in_=x_sb[:, m, K_PASS * g : K_PASS * (g + 1)].rearrange("n (p t) -> n t p", t=PACK),
                    func=ACT.Identity,
                    scale=rstd[:, m : m + 1],
                    bias=shift[:, m : m + 1],
                )
        ln_col = const.tile([P, PACK, 16], F32, name="ln_col")
        nc.scalar.copy(out=ln_col[:], in_=params_ps[:, 0:PACK, 0:16])
        b1_col = const.tile([P, HEADS * H // P], F32, name="b1_col")
        nc.scalar.copy(out=b1_col[:], in_=params_ps[:, PACK, 0 : HEADS * H // P])

        xn_t = {}
        for g in range(PASSES):
            for t in range(PACK):
                if t % 2 == 0:
                    pool, tag = (sum_pool, "sums") if (g, t) == (1, 2) else (turn_pool, "turned")
                    xn_t[(g, t // 2)] = pool.tile([P, 2, TOK], F32, name="xn_t%d_%d" % (g, t // 2), tag=tag)
                for m in range(TOK_TILES):
                    nc.tensor.transpose(
                        out=xn_t[(g, t // 2)][:, t % 2, m * P : (m + 1) * P],
                        in_=xn[:, m, g, t, :],
                        identity=ident[:],
                    )

        y_words = const.tile([P, HEADS, PASSES * TOK], U32, name="y_words", align_bytes=64)
        y_scales = const.tile([P, HEADS, PASSES * TOK], U8, name="y_scales", align_bytes=64)
        y_planes, y_grouped = {}, {}

        def affine(k):
            y_planes[k] = y_pool.tile([P, PASSES, PACK, TOK], BF16, name="y_planes%d" % k, tag="y_planes")
            for g in range(PASSES):
                for t in range(PACK):
                    row = PASSES * k + g
                    nc.scalar.activation(
                        out=y_planes[k][:, g, t, :],
                        in_=xn_t[(g, t // 2)][:, t % 2, :],
                        func=ACT.Identity,
                        scale=ln_col[:, t, row : row + 1],
                        bias=ln_col[:, t, 8 + row : 8 + row + 1],
                    )

        def y_regroup(k):
            y_grouped[k] = y_pool.tile([P, PASSES, TOK, PACK], BF16, name="y_grouped%d" % k, tag="y_grouped", align_bytes=64)
            for g in range(PASSES):
                nc.vector.tensor_copy(
                    out=y_grouped[k][:, g].rearrange("p (c i) t -> p c t i", i=4),
                    in_=y_planes[k][:, g].rearrange("p t (c i) -> p c t i", i=4),
                )

        def y_quantise(k):
            nc.vector.quantize_mx(
                out=y_words[:, k, :].bitcast(FP8X4),
                scales=y_scales[:, k, :],
                in_=y_grouped[k][:].rearrange("p g n t -> p (g n t)"),
            )

        regroup(1)
        quantise(0)
        for k in range(HEADS):
            affine(k)
            regroup(k + 2)
            if k + 2 >= TENSOR_FROM:
                regroup_on_tensor(k + 2)
                copy_bank(k + 2)
            if k == 1:
                load_w(3)
                b1_row = const.tile([P, (ROUNDS - TOKENS_FROM) * COLS], BF16, name="b1_row")
                nc.sync.dma_start(out=b1_row[:], in_=b1[HEADS - 1, H - (ROUNDS - TOKENS_FROM) * COLS :].partition_broadcast(P))
            if k >= 1:
                y_quantise(k - 1)
            quantise(k + 1)
            y_regroup(k)
            if k == 1:
                multiply(0)
        regroup(HEADS + 2)
        if HEADS + 2 >= TENSOR_FROM:
            regroup_on_tensor(HEADS + 2)
        y_quantise(HEADS - 1)

        for i in range(ROUNDS):
            if 1 <= i <= TOKENS_FROM:
                turn_back(i - 1)
            on_tensor = max(PROLOGUE_REGROUPED, TENSOR_FROM) <= i + LEAD < ROUNDS
            if PROLOGUE_REGROUPED <= i + LEAD < ROUNDS:
                regroup(i + LEAD)
            if i + 1 < ROUNDS:
                multiply(i + 1)
            if on_tensor:
                regroup_on_tensor(i + LEAD)
            if PROLOGUE_QUANTISED <= i + LEAD - 1 < ROUNDS:
                quantise(i + LEAD - 1)
            if i < TOKENS_FROM:
                bias_gelu(i)
            if i == 0:
                copy_bank(HEADS + 2)
            if 1 <= i <= TOKENS_FROM:
                copy_out_and_store(i - 1)
            if i >= TOKENS_FROM:
                add_gelu_and_store(i)
            if on_tensor:
                copy_bank(i + LEAD)
